import numpy as np
import ml_dtypes


def mxq(x, axis, fmt="e4m3"):
    dtype, down = {"e4m3": (ml_dtypes.float8_e4m3fn, 7), "e5m2": (ml_dtypes.float8_e5m2, 14)}[fmt]
    v = np.moveaxis(np.asarray(x, np.float32).astype(ml_dtypes.bfloat16).astype(np.float64), axis, -1)
    blocks = v.reshape(v.shape[:-1] + (-1, 32))
    amax = np.abs(blocks).max(-1, keepdims=True)
    byte = np.maximum(np.where(amax > 0, np.frexp(amax)[1] - 1 + 127, 0) - down, 1)
    scale = np.exp2(byte - 127.0)
    codes = (blocks / scale).astype(np.float32).astype(dtype).astype(np.float64)
    return np.moveaxis((codes * scale).reshape(v.shape), -1, axis)


WIDE = False


def mx_kscale(k):
    if not WIDE:
        return np.ones(k)
    levels = np.array([10, -10, 5, -5, 0])
    a = np.random.permutation(np.resize(levels, k // 512 * 4)).reshape(k // 512, 4)
    idx = np.arange(k)
    return np.exp2(a[idx // 512, idx % 128 // 32])


BF16 = ml_dtypes.bfloat16


def bf(x):
    return np.asarray(x, np.float32).astype(BF16)


def f64(x):
    return np.asarray(x).astype(np.float64)


W, S, K, T, D = 8, 128, 8, 128, 512
LN_EPS = 1e-5


def layer_norm(x, gamma, beta):
    mu = x.mean(-1, keepdims=True)
    var = np.square(x - mu).mean(-1, keepdims=True)
    return (x - mu) / np.sqrt(var + LN_EPS) * gamma + beta


def setup_inputs():
    n = np.random.standard_normal
    s = mx_kscale(D)
    shot_bias = np.repeat(np.log(np.random.uniform(0.05, 1.0, (W, K))), T, axis=1)
    return {"logits": bf(n((W, S, K * T)) * 1.5 + shot_bias[:, None, :]),
            "support_transport": bf(n((W, K, T, D)) * s),
            "Wv": bf(n((D, D)) * 1.5 / np.sqrt(D) / s[None, :]),
            "class_slots": bf(n((W, S, D)) * 0.5),
            "g_out": bf(1.0 + 0.1 * n(D)),
            "b_out": bf(0.1 * n(D))}


def reference(logits, support_transport, Wv, class_slots, g_out, b_out):
    flat = f64(support_transport).reshape(W, K * T, D)
    v = mxq(flat, 2, "e4m3") @ mxq(f64(Wv), 1, "e4m3").T
    l = f64(logits)
    e = np.exp(l - l.max(-1, keepdims=True))
    mem = (mxq(e, 2, "e4m3") @ mxq(v, 1, "e4m3")) / e.sum(-1, keepdims=True)
    return layer_norm(f64(class_slots) + mem, f64(g_out), f64(b_out))

@@ -1,0 +1,267 @@
+from contextlib import ExitStack
+
+import concourse.mybir as mybir
+from concourse.masks import make_identity
+
+F32 = mybir.dt.float32
+BF16 = mybir.dt.bfloat16
+U32 = mybir.dt.uint32
+U8 = mybir.dt.uint8
+FP8X4 = mybir.dt.float8_e4m3fn_x4
+ALU = mybir.AluOpType
+ACT = mybir.ActivationFunctionType
+
+P = 128
+PACK = 4
+K_PASS = P * PACK
+PAIR = 2
+
+CLASSES = 8
+SLOTS = 128
+TOKENS = 1024
+FEATURES = 512
+LN_EPS = 1e-5
+
+UNIT_TOKENS = K_PASS
+UNITS_PER_CLASS = TOKENS // UNIT_TOKENS
+UNITS = CLASSES * UNITS_PER_CLASS
+FEATURE_CHUNKS = FEATURES // P
+WORD_HALVES = FEATURES // PAIR // P
+
+PSUM_BUFS = {"ft": 2, "v": 4, "eT": 1, "mem": 1}
+
+FLOPS = 2 * CLASSES * TOKENS * FEATURES * FEATURES + 2 * CLASSES * SLOTS * TOKENS * FEATURES
+
+
+def tile_consensustransportmemorypool_pb_t_kernel(
+    tc, logits, support_transport, Wv, class_slots, g_out, b_out, out
+):
+    nc = tc.nc
+    with ExitStack() as ctx:
+        consts = ctx.enter_context(tc.tile_pool(name="consts", bufs=1))
+        inputs = ctx.enter_context(tc.tile_pool(name="inputs", bufs=1))
+        work = ctx.enter_context(tc.tile_pool(name="work", bufs=2))
+        stats = ctx.enter_context(tc.tile_pool(name="stats", bufs=4))
+        results = ctx.enter_context(tc.tile_pool(name="results", bufs=CLASSES))
+        psum = ctx.enter_context(tc.psum_pool(name="psum", bufs=1))
+
+        ident_f32 = consts.tile([P, P], F32)
+        make_identity(nc, ident_f32[:])
+        ident_bf16 = consts.tile([P, P], BF16)
+        make_identity(nc, ident_bf16[:])
+        minus_half = consts.tile([P, 1], F32)
+        nc.gpsimd.memset(minus_half[:], -0.5)
+        ones = consts.tile([P, P], BF16)
+        nc.vector.memset(ones[:], 1.0)
+        affine_rows = consts.tile([P, 2 * FEATURES], BF16)
+        nc.vector.memset(affine_rows[:], 0.0)
+        nc.scalar.dma_start(out=affine_rows[0:1, 0:FEATURES], in_=g_out.rearrange("(o d) -> o d", o=1))
+        nc.scalar.dma_start(out=affine_rows[0:1, FEATURES : 2 * FEATURES], in_=b_out.rearrange("(o d) -> o d", o=1))
+
+        tokens = support_transport.rearrange("w k t f -> w (k t) f")
+        logits_sb = {}
+        flat_sb = {}
+
+        def load_logits(c):
+            logits_sb[c] = inputs.tile([P, TOKENS], BF16, name="logits%d" % c)
+            nc.sync.dma_start(out=logits_sb[c][:], in_=logits[c, :, :])
+
+        def load_flat(h):
+            c, g = divmod(h, UNITS_PER_CLASS)
+            flat_sb[h] = inputs.tile([P, PACK * FEATURES], BF16, name="flat%d" % h)
+            rows = tokens[c, g * UNIT_TOKENS : (g + 1) * UNIT_TOKENS, :]
+            nc.sync.dma_start(out=flat_sb[h][:], in_=rows.rearrange("(p j) f -> p (j f)", j=PACK))
+
+        load_logits(0)
+        wv_sb = inputs.tile([P, FEATURE_CHUNKS * FEATURES], BF16)
+        nc.sync.dma_start(
+            out=wv_sb[:].rearrange("p (o k) -> p o k", o=FEATURE_CHUNKS),
+            in_=Wv.rearrange("(o p) k -> p o k", p=P),
+        )
+        load_flat(0)
+        load_flat(1)
+        load_logits(1)
+        load_flat(2)
+        load_flat(3)
+        slots_sb = inputs.tile([P, CLASSES, FEATURES], BF16)
+        nc.sync.dma_start(out=slots_sb[:], in_=class_slots.rearrange("w s d -> s w d"))
+        for c in range(2, CLASSES):
+            load_logits(c)
+            load_flat(UNITS_PER_CLASS * c)
+            load_flat(UNITS_PER_CLASS * c + 1)
+
+        def transpose_words(rows_sb, first_block, tag):
+            words = rows_sb[:].bitcast(F32)
+            bank = psum.tile([P, 2, WORD_HALVES, P], F32, tag=tag, bufs=PSUM_BUFS[tag])
+            for b in range(2):
+                for u in range(WORD_HALVES):
+                    col = ((first_block + b) * WORD_HALVES + u) * P
+                    nc.tensor.transpose(bank[:, b, u, :], words[:, col : col + P], ident_f32[:])
+            return bank
+
+        def regroup_words(copy, grouped, first_block, bank):
+            words = grouped[:].bitcast(F32).rearrange("q (b r u) -> q b r u", r=P, u=WORD_HALVES)
+            copy(out=words[:, first_block : first_block + 2, :, :], in_=bank[:].rearrange("q b u r -> q b r u"))
+
+        flat_banks = {}
+        flat_grouped = {}
+
+        def transpose_flat(h):
+            flat_banks[h] = [transpose_words(flat_sb[h], first, "ft") for first in (0, 2)]
+
+        def regroup_flat(h):
+            flat_grouped[h] = work.tile([P, PACK * UNIT_TOKENS], BF16, name="flat_grouped", align_bytes=64)
+            for half, first in enumerate((0, 2)):
+                last_of_class = h % UNITS_PER_CLASS == UNITS_PER_CLASS - 1 and half == 1
+                copy = nc.scalar.copy if last_of_class else nc.vector.tensor_copy
+                regroup_words(copy, flat_grouped[h], first, flat_banks[h][half])
+
+        v_grouped = {}
+
+        def project(h):
+            flat_codes = work.tile([P, UNIT_TOKENS], U32, align_bytes=64)
+            flat_scales = work.tile([P, UNIT_TOKENS], U8, align_bytes=64)
+            nc.vector.quantize_mx(out=flat_codes[:].bitcast(FP8X4), scales=flat_scales[:], in_=flat_grouped[h][:])
+            v_grouped[h] = work.tile([P, PACK * FEATURES], BF16, name="v_grouped", bufs=3, align_bytes=64)
+            chunks = v_grouped[h][:].rearrange("p (c d j) -> p c d j", c=FEATURE_CHUNKS, j=PACK)
+            for chunk in range(FEATURE_CHUNKS):
+                d_cols = slice(chunk * P, (chunk + 1) * P)
+                bank = psum.tile([P, PACK, P], F32, tag="v", bufs=PSUM_BUFS["v"])
+                for j in range(PACK):
+                    t_cols = slice(j * P, (j + 1) * P)
+                    nc.tensor.matmul_mx(
+                        out=bank[:, j, :],
+                        lhsT=flat_codes[:, t_cols].bitcast(FP8X4),
+                        lhsT_scale=flat_scales[:, t_cols],
+                        rhs=wv_codes[:, d_cols].bitcast(FP8X4),
+                        rhs_scale=wv_scales[:, d_cols],
+                        start=True,
+                        stop=True,
+                    )
+                nc.scalar.copy(out=chunks[:, chunk, :, :], in_=bank[:].rearrange("p j d -> p d j"))
+
+        e_grouped = {}
+        e_codes = {}
+        e_scales = {}
+        e_sb = {}
+        row_sum = {}
+        mem_bank = {}
+
+        def softmax_weights(c):
+            neg_max = stats.tile([P, 1], F32)
+            neg_logits = work.tile([P, TOKENS], BF16)
+            nc.vector.tensor_scalar(
+                out=neg_logits[:],
+                in0=logits_sb[c][:],
+                scalar1=-1.0,
+                scalar2=None,
+                op0=ALU.mult,
+                op1=ALU.min,
+                accum_out=neg_max[:],
+            )
+            row_sum[c] = stats.tile([P, 1], F32, name="row_sum")
+            e_sb[c] = work.tile([P, UNITS_PER_CLASS, PACK, P], BF16, name="e_sb")
+            nc.scalar.activation(
+                out=e_sb[c][:].rearrange("s g j p -> s g p j"),
+                in_=logits_sb[c][:].rearrange("s (g p j) -> s g p j", g=UNITS_PER_CLASS, j=PACK),
+                func=ACT.Exp,
+                bias=neg_max[:],
+                scale=1.0,
+                accum_out=row_sum[c][:],
+            )
+
+        def transpose_weights(c):
+            bank = psum.tile([P, UNITS_PER_CLASS, PACK, SLOTS], BF16, tag="eT", bufs=PSUM_BUFS["eT"])
+            for g in range(UNITS_PER_CLASS):
+                for j in range(PACK):
+                    nc.tensor.transpose(bank[:, g, j, :], e_sb[c][:, g, j, :], ident_bf16[:])
+            e_grouped[c] = work.tile([P, UNITS_PER_CLASS, SLOTS, PACK], BF16, name="e_grouped", align_bytes=64)
+            nc.scalar.copy(out=e_grouped[c][:], in_=bank[:].rearrange("p g j s -> p g s j"))
+
+        def quantise_weights(c):
+            e_codes[c] = work.tile([P, UNITS_PER_CLASS * SLOTS], U32, name="e_codes", align_bytes=64)
+            e_scales[c] = work.tile([P, UNITS_PER_CLASS * SLOTS], U8, name="e_scales", align_bytes=64)
+            nc.vector.quantize_mx(
+                out=e_codes[c][:].bitcast(FP8X4),
+                scales=e_scales[c][:],
+                in_=e_grouped[c][:].rearrange("p g s j -> p (g s j)"),
+            )
+
+        def pool_unit(h):
+            c, g = divmod(h, UNITS_PER_CLASS)
+            if g == 0:
+                quantise_weights(c)
+                mem_bank[c] = psum.tile([P, FEATURES], F32, name="mem_bank", tag="mem", bufs=PSUM_BUFS["mem"])
+            v_codes = work.tile([P, FEATURES], U32, align_bytes=64)
+            v_scales = work.tile([P, FEATURES], U8, align_bytes=64)
+            nc.vector.quantize_mx(out=v_codes[:].bitcast(FP8X4), scales=v_scales[:], in_=v_grouped[h][:])
+            s_cols = slice(g * SLOTS, (g + 1) * SLOTS)
+            nc.tensor.matmul_mx(
+                out=mem_bank[c][:],
+                lhsT=e_codes[c][:, s_cols].bitcast(FP8X4),
+                lhsT_scale=e_scales[c][:, s_cols],
+                rhs=v_codes[:].bitcast(FP8X4),
+                rhs_scale=v_scales[:],
+                start=(g == 0),
+                stop=(g == UNITS_PER_CLASS - 1),
+            )
+
+        centred = {}
+        rstd = {}
+
+        def norm_start(c):
+            inv_sum = stats.tile([P, 1], F32)
+            nc.vector.reciprocal(out=inv_sum[:], in_=row_sum[c][:])
+            y = work.tile([P, FEATURES], F32)
+            nc.vector.scalar_tensor_tensor(
+                out=y[:], in0=mem_bank[c][:], scalar=inv_sum[:], in1=slots_sb[:, c, :], op0=ALU.mult, op1=ALU.add
+            )
+            moments = stats.tile([P, 6], F32)
+            nc.vector.bn_stats(out=moments[:], in_=y[:])
+            mean_var = stats.tile([P, 2], F32)
+            nc.vector.bn_aggr(out=mean_var[:], in_=moments[:])
+            var_eps = stats.tile([P, 1], F32)
+            nc.gpsimd.tensor_scalar(
+                out=var_eps[:], in0=mean_var[:, 1:2], scalar1=LN_EPS, scalar2=1.0, op0=ALU.add, op1=ALU.mult
+            )
+            rstd[c] = stats.tile([P, 1], F32, name="rstd")
+            nc.gpsimd.tensor_tensor(out=rstd[c][:], in0=var_eps[:], in1=minus_half[:], op=ALU.pow)
+            centred[c] = work.tile([P, FEATURES], F32, name="centred")
+            nc.vector.scalar_tensor_tensor(
+                out=centred[c][:], in0=y[:], scalar=mean_var[:, 0:1], in1=gain[:], op0=ALU.subtract, op1=ALU.mult
+            )
+
+        def norm_finish(c):
+            result = results.tile([P, FEATURES], F32)
+            nc.vector.scalar_tensor_tensor(
+                out=result[:], in0=centred[c][:], scalar=rstd[c][:], in1=shift[:], op0=ALU.mult, op1=ALU.add
+            )
+            nc.sync.dma_start(out=out[c, :, :], in_=result[:])
+
+        wv_grouped = consts.tile([P, PACK * FEATURES], BF16, align_bytes=64)
+        for first in (0, 2):
+            regroup_words(nc.scalar.copy, wv_grouped, first, transpose_words(wv_sb, first, "v"))
+        wv_codes = consts.tile([P, FEATURES], U32, align_bytes=64)
+        wv_scales = consts.tile([P, FEATURES], U8, align_bytes=64)
+        nc.vector.quantize_mx(out=wv_codes[:].bitcast(FP8X4), scales=wv_scales[:], in_=wv_grouped[:])
+        gain = consts.tile([P, FEATURES], F32)
+        shift = consts.tile([P, FEATURES], F32)
+        for i, spread in enumerate((gain, shift)):
+            bank = psum.tile([P, FEATURES], F32, tag="v", bufs=PSUM_BUFS["v"])
+            nc.tensor.matmul(
+                out=bank[:], lhsT=ones[:], rhs=affine_rows[:, i * FEATURES : (i + 1) * FEATURES], start=True, stop=True
+            )
+            nc.scalar.copy(out=spread[:], in_=bank[:])
+
+        for c in range(CLASSES):
+            units = range(UNITS_PER_CLASS * c, UNITS_PER_CLASS * (c + 1))
+            softmax_weights(c)
+            transpose_weights(c)
+            for h in units:
+                transpose_flat(h)
+                regroup_flat(h)
+                project(h)
+            for h in units:
+                pool_unit(h)
+            norm_start(c)
+            norm_finish(c)

@@ -28,6 +28,8 @@ UNITS = CLASSES * UNITS_PER_CLASS
 FEATURE_CHUNKS = FEATURES // P
 WORD_HALVES = FEATURES // PAIR // P
 
+CLOCK_COLS = 256
+
 PSUM_BUFS = {"ft": 2, "v": 4, "eT": 1, "mem": 1}
 
 FLOPS = 2 * CLASSES * TOKENS * FEATURES * FEATURES + 2 * CLASSES * SLOTS * TOKENS * FEATURES
@@ -127,6 +129,15 @@ def tile_consensustransportmemorypool_pb_t_kernel(
             for chunk in range(FEATURE_CHUNKS):
                 d_cols = slice(chunk * P, (chunk + 1) * P)
                 bank = psum.tile([P, PACK, P], F32, tag="v", bufs=PSUM_BUFS["v"])
+                nc.tensor.matmul_mx(
+                    out=bank[:].rearrange("p j d -> p (j d)")[:, 0:CLOCK_COLS],
+                    lhsT=flat_codes[:, 0:P].bitcast(FP8X4),
+                    lhsT_scale=flat_scales[:, 0:P],
+                    rhs=wv_codes[:, 0:CLOCK_COLS].bitcast(FP8X4),
+                    rhs_scale=wv_scales[:, 0:CLOCK_COLS],
+                    start=True,
+                    stop=True,
+                )
                 for j in range(PACK):
                     t_cols = slice(j * P, (j + 1) * P)
                     nc.tensor.matmul_mx(

@@ -28,8 +28,6 @@ UNITS = CLASSES * UNITS_PER_CLASS
 FEATURE_CHUNKS = FEATURES // P
 WORD_HALVES = FEATURES // PAIR // P
 
-CLOCK_COLS = 256
-
 PSUM_BUFS = {"ft": 2, "v": 4, "eT": 1, "mem": 1}
 
 FLOPS = 2 * CLASSES * TOKENS * FEATURES * FEATURES + 2 * CLASSES * SLOTS * TOKENS * FEATURES
@@ -40,6 +38,7 @@ def tile_consensustransportmemorypool_pb_t_kernel(
 ):
     nc = tc.nc
     with ExitStack() as ctx:
+        ctx.enter_context(tc.manual_schedule())
         consts = ctx.enter_context(tc.tile_pool(name="consts", bufs=1))
         inputs = ctx.enter_context(tc.tile_pool(name="inputs", bufs=1))
         work = ctx.enter_context(tc.tile_pool(name="work", bufs=2))
@@ -107,6 +106,8 @@ def tile_consensustransportmemorypool_pb_t_kernel(
 
         flat_banks = {}
         flat_grouped = {}
+        flat_codes = {}
+        flat_scales = {}
 
         def transpose_flat(h):
             flat_banks[h] = [transpose_words(flat_sb[h], first, "ft") for first in (0, 2)]
@@ -114,52 +115,62 @@ def tile_consensustransportmemorypool_pb_t_kernel(
         def regroup_flat(h):
             flat_grouped[h] = work.tile([P, PACK * UNIT_TOKENS], BF16, name="flat_grouped", align_bytes=64)
             for half, first in enumerate((0, 2)):
-                last_of_class = h % UNITS_PER_CLASS == UNITS_PER_CLASS - 1 and half == 1
-                copy = nc.scalar.copy if last_of_class else nc.vector.tensor_copy
+                scalar_share = h >= UNITS_PER_CLASS and h % UNITS_PER_CLASS == 0 and half == 1
+                copy = nc.scalar.copy if scalar_share else nc.vector.tensor_copy
                 regroup_words(copy, flat_grouped[h], first, flat_banks[h][half])
 
+        def quantise_flat(h):
+            flat_codes[h] = work.tile([P, UNIT_TOKENS], U32, name="flat_codes", align_bytes=64)
+            flat_scales[h] = work.tile([P, UNIT_TOKENS], U8, name="flat_scales", align_bytes=64)
+            nc.vector.quantize_mx(
+                out=flat_codes[h][:].bitcast(FP8X4), scales=flat_scales[h][:], in_=flat_grouped[h][:]
+            )
+
+        v_banks = {}
         v_grouped = {}
+        v_codes = {}
+        v_scales = {}
 
         def project(h):
-            flat_codes = work.tile([P, UNIT_TOKENS], U32, align_bytes=64)
-            flat_scales = work.tile([P, UNIT_TOKENS], U8, align_bytes=64)
-            nc.vector.quantize_mx(out=flat_codes[:].bitcast(FP8X4), scales=flat_scales[:], in_=flat_grouped[h][:])
-            v_grouped[h] = work.tile([P, PACK * FEATURES], BF16, name="v_grouped", bufs=3, align_bytes=64)
-            chunks = v_grouped[h][:].rearrange("p (c d j) -> p c d j", c=FEATURE_CHUNKS, j=PACK)
+            v_banks[h] = []
             for chunk in range(FEATURE_CHUNKS):
                 d_cols = slice(chunk * P, (chunk + 1) * P)
                 bank = psum.tile([P, PACK, P], F32, tag="v", bufs=PSUM_BUFS["v"])
-                nc.tensor.matmul_mx(
-                    out=bank[:].rearrange("p j d -> p (j d)")[:, 0:CLOCK_COLS],
-                    lhsT=flat_codes[:, 0:P].bitcast(FP8X4),
-                    lhsT_scale=flat_scales[:, 0:P],
-                    rhs=wv_codes[:, 0:CLOCK_COLS].bitcast(FP8X4),
-                    rhs_scale=wv_scales[:, 0:CLOCK_COLS],
-                    start=True,
-                    stop=True,
-                )
                 for j in range(PACK):
                     t_cols = slice(j * P, (j + 1) * P)
                     nc.tensor.matmul_mx(
                         out=bank[:, j, :],
-                        lhsT=flat_codes[:, t_cols].bitcast(FP8X4),
-                        lhsT_scale=flat_scales[:, t_cols],
+                        lhsT=flat_codes[h][:, t_cols].bitcast(FP8X4),
+                        lhsT_scale=flat_scales[h][:, t_cols],
                         rhs=wv_codes[:, d_cols].bitcast(FP8X4),
                         rhs_scale=wv_scales[:, d_cols],
                         start=True,
                         stop=True,
                     )
-                nc.scalar.copy(out=chunks[:, chunk, :, :], in_=bank[:].rearrange("p j d -> p d j"))
+                v_banks[h].append(bank)
 
+        def regroup_v(h):
+            v_grouped[h] = work.tile([P, PACK * FEATURES], BF16, name="v_grouped", bufs=3, align_bytes=64)
+            chunks = v_grouped[h][:].rearrange("p (c d j) -> p c d j", c=FEATURE_CHUNKS, j=PACK)
+            for chunk in range(FEATURE_CHUNKS):
+                nc.scalar.copy(out=chunks[:, chunk, :, :], in_=v_banks[h][chunk][:].rearrange("p j d -> p d j"))
+
+        def quantise_v(h):
+            v_codes[h] = work.tile([P, FEATURES], U32, name="v_codes", align_bytes=64)
+            v_scales[h] = work.tile([P, FEATURES], U8, name="v_scales", align_bytes=64)
+            nc.vector.quantize_mx(out=v_codes[h][:].bitcast(FP8X4), scales=v_scales[h][:], in_=v_grouped[h][:])
+
+        neg_max = {}
+        row_sum = {}
+        e_sb = {}
+        e_bank = {}
         e_grouped = {}
         e_codes = {}
         e_scales = {}
-        e_sb = {}
-        row_sum = {}
         mem_bank = {}
 
-        def softmax_weights(c):
-            neg_max = stats.tile([P, 1], F32)
+        def row_max(c):
+            neg_max[c] = stats.tile([P, 1], F32, name="neg_max")
             neg_logits = work.tile([P, TOKENS], BF16)
             nc.vector.tensor_scalar(
                 out=neg_logits[:],
@@ -168,26 +179,30 @@ def tile_consensustransportmemorypool_pb_t_kernel(
                 scalar2=None,
                 op0=ALU.mult,
                 op1=ALU.min,
-                accum_out=neg_max[:],
+                accum_out=neg_max[c][:],
             )
+
+        def exponentials(c):
             row_sum[c] = stats.tile([P, 1], F32, name="row_sum")
             e_sb[c] = work.tile([P, UNITS_PER_CLASS, PACK, P], BF16, name="e_sb")
             nc.scalar.activation(
                 out=e_sb[c][:].rearrange("s g j p -> s g p j"),
                 in_=logits_sb[c][:].rearrange("s (g p j) -> s g p j", g=UNITS_PER_CLASS, j=PACK),
                 func=ACT.Exp,
-                bias=neg_max[:],
+                bias=neg_max[c][:],
                 scale=1.0,
                 accum_out=row_sum[c][:],
             )
 
         def transpose_weights(c):
-            bank = psum.tile([P, UNITS_PER_CLASS, PACK, SLOTS], BF16, tag="eT", bufs=PSUM_BUFS["eT"])
+            e_bank[c] = psum.tile([P, UNITS_PER_CLASS, PACK, SLOTS], BF16, name="e_bank", tag="eT", bufs=PSUM_BUFS["eT"])
             for g in range(UNITS_PER_CLASS):
                 for j in range(PACK):
-                    nc.tensor.transpose(bank[:, g, j, :], e_sb[c][:, g, j, :], ident_bf16[:])
+                    nc.tensor.transpose(e_bank[c][:, g, j, :], e_sb[c][:, g, j, :], ident_bf16[:])
+
+        def regroup_weights(c):
             e_grouped[c] = work.tile([P, UNITS_PER_CLASS, SLOTS, PACK], BF16, name="e_grouped", align_bytes=64)
-            nc.scalar.copy(out=e_grouped[c][:], in_=bank[:].rearrange("p g j s -> p g s j"))
+            nc.scalar.copy(out=e_grouped[c][:], in_=e_bank[c][:].rearrange("p g j s -> p g s j"))
 
         def quantise_weights(c):
             e_codes[c] = work.tile([P, UNITS_PER_CLASS * SLOTS], U32, name="e_codes", align_bytes=64)
@@ -201,45 +216,45 @@ def tile_consensustransportmemorypool_pb_t_kernel(
         def pool_unit(h):
             c, g = divmod(h, UNITS_PER_CLASS)
             if g == 0:
-                quantise_weights(c)
                 mem_bank[c] = psum.tile([P, FEATURES], F32, name="mem_bank", tag="mem", bufs=PSUM_BUFS["mem"])
-            v_codes = work.tile([P, FEATURES], U32, align_bytes=64)
-            v_scales = work.tile([P, FEATURES], U8, align_bytes=64)
-            nc.vector.quantize_mx(out=v_codes[:].bitcast(FP8X4), scales=v_scales[:], in_=v_grouped[h][:])
             s_cols = slice(g * SLOTS, (g + 1) * SLOTS)
             nc.tensor.matmul_mx(
                 out=mem_bank[c][:],
                 lhsT=e_codes[c][:, s_cols].bitcast(FP8X4),
                 lhsT_scale=e_scales[c][:, s_cols],
-                rhs=v_codes[:].bitcast(FP8X4),
-                rhs_scale=v_scales[:],
+                rhs=v_codes[h][:].bitcast(FP8X4),
+                rhs_scale=v_scales[h][:],
                 start=(g == 0),
                 stop=(g == UNITS_PER_CLASS - 1),
             )
 
-        centred = {}
+        y = {}
+        mean_var = {}
         rstd = {}
+        centred = {}
 
-        def norm_start(c):
+        def norm_stats(c):
             inv_sum = stats.tile([P, 1], F32)
             nc.vector.reciprocal(out=inv_sum[:], in_=row_sum[c][:])
-            y = work.tile([P, FEATURES], F32)
+            y[c] = work.tile([P, FEATURES], F32, name="y")
             nc.vector.scalar_tensor_tensor(
-                out=y[:], in0=mem_bank[c][:], scalar=inv_sum[:], in1=slots_sb[:, c, :], op0=ALU.mult, op1=ALU.add
+                out=y[c][:], in0=mem_bank[c][:], scalar=inv_sum[:], in1=slots_sb[:, c, :], op0=ALU.mult, op1=ALU.add
             )
             moments = stats.tile([P, 6], F32)
-            nc.vector.bn_stats(out=moments[:], in_=y[:])
-            mean_var = stats.tile([P, 2], F32)
-            nc.vector.bn_aggr(out=mean_var[:], in_=moments[:])
+            nc.vector.bn_stats(out=moments[:], in_=y[c][:])
+            mean_var[c] = stats.tile([P, 2], F32, name="mean_var")
+            nc.vector.bn_aggr(out=mean_var[c][:], in_=moments[:])
             var_eps = stats.tile([P, 1], F32)
             nc.gpsimd.tensor_scalar(
-                out=var_eps[:], in0=mean_var[:, 1:2], scalar1=LN_EPS, scalar2=1.0, op0=ALU.add, op1=ALU.mult
+                out=var_eps[:], in0=mean_var[c][:, 1:2], scalar1=LN_EPS, scalar2=1.0, op0=ALU.add, op1=ALU.mult
             )
             rstd[c] = stats.tile([P, 1], F32, name="rstd")
             nc.gpsimd.tensor_tensor(out=rstd[c][:], in0=var_eps[:], in1=minus_half[:], op=ALU.pow)
+
+        def norm_centre(c):
             centred[c] = work.tile([P, FEATURES], F32, name="centred")
             nc.vector.scalar_tensor_tensor(
-                out=centred[c][:], in0=y[:], scalar=mean_var[:, 0:1], in1=gain[:], op0=ALU.subtract, op1=ALU.mult
+                out=centred[c][:], in0=y[c][:], scalar=mean_var[c][:, 0:1], in1=gain[:], op0=ALU.subtract, op1=ALU.mult
             )
 
         def norm_finish(c):
@@ -249,12 +264,18 @@ def tile_consensustransportmemorypool_pb_t_kernel(
             )
             nc.sync.dma_start(out=out[c, :, :], in_=result[:])
 
+        row_max(0)
+        exponentials(0)
         wv_grouped = consts.tile([P, PACK * FEATURES], BF16, align_bytes=64)
         for first in (0, 2):
             regroup_words(nc.scalar.copy, wv_grouped, first, transpose_words(wv_sb, first, "v"))
+        transpose_flat(0)
+        regroup_flat(0)
+        transpose_flat(1)
         wv_codes = consts.tile([P, FEATURES], U32, align_bytes=64)
         wv_scales = consts.tile([P, FEATURES], U8, align_bytes=64)
         nc.vector.quantize_mx(out=wv_codes[:].bitcast(FP8X4), scales=wv_scales[:], in_=wv_grouped[:])
+        quantise_flat(0)
         gain = consts.tile([P, FEATURES], F32)
         shift = consts.tile([P, FEATURES], F32)
         for i, spread in enumerate((gain, shift)):
@@ -263,16 +284,39 @@ def tile_consensustransportmemorypool_pb_t_kernel(
                 out=bank[:], lhsT=ones[:], rhs=affine_rows[:, i * FEATURES : (i + 1) * FEATURES], start=True, stop=True
             )
             nc.scalar.copy(out=spread[:], in_=bank[:])
+        project(0)
+        transpose_weights(0)
+        regroup_flat(1)
+        transpose_flat(2)
 
-        for c in range(CLASSES):
-            units = range(UNITS_PER_CLASS * c, UNITS_PER_CLASS * (c + 1))
-            softmax_weights(c)
-            transpose_weights(c)
-            for h in units:
-                transpose_flat(h)
-                regroup_flat(h)
-                project(h)
-            for h in units:
-                pool_unit(h)
-            norm_start(c)
-            norm_finish(c)
+        for i in range(UNITS + 3):
+            odd = i % UNITS_PER_CLASS == 1
+            if i < UNITS:
+                regroup_v(i)
+            if i + 1 < UNITS:
+                quantise_flat(i + 1)
+            if 1 <= i <= UNITS:
+                if odd:
+                    quantise_weights((i - 1) // UNITS_PER_CLASS)
+                quantise_v(i - 1)
+            if i + 1 < UNITS:
+                project(i + 1)
+            if odd and 0 <= (i - 3) // UNITS_PER_CLASS < CLASSES:
+                norm_stats((i - 3) // UNITS_PER_CLASS)
+            if not odd and 0 <= (i - 4) // UNITS_PER_CLASS < CLASSES:
+                norm_finish((i - 4) // UNITS_PER_CLASS)
+            if not odd and i // UNITS_PER_CLASS + 1 < CLASSES:
+                row_max(i // UNITS_PER_CLASS + 1)
+            if 1 <= i <= UNITS:
+                pool_unit(i - 1)
+            if i + 2 < UNITS:
+                regroup_flat(i + 2)
+            if i + 3 < UNITS:
+                transpose_flat(i + 3)
+            if odd and (i + 1) // UNITS_PER_CLASS < CLASSES:
+                exponentials((i + 1) // UNITS_PER_CLASS)
+                transpose_weights((i + 1) // UNITS_PER_CLASS)
+            if not odd and i // UNITS_PER_CLASS < CLASSES:
+                regroup_weights(i // UNITS_PER_CLASS)
+            if odd and 0 <= (i - 3) // UNITS_PER_CLASS < CLASSES:
+                norm_centre((i - 3) // UNITS_PER_CLASS)

@@ -52,12 +52,6 @@ def tile_consensustransportmemorypool_pb_t_kernel(
         make_identity(nc, ident_bf16[:])
         minus_half = consts.tile([P, 1], F32)
         nc.gpsimd.memset(minus_half[:], -0.5)
-        ones = consts.tile([P, P], BF16)
-        nc.vector.memset(ones[:], 1.0)
-        affine_rows = consts.tile([P, 2 * FEATURES], BF16)
-        nc.vector.memset(affine_rows[:], 0.0)
-        nc.scalar.dma_start(out=affine_rows[0:1, 0:FEATURES], in_=g_out.rearrange("(o d) -> o d", o=1))
-        nc.scalar.dma_start(out=affine_rows[0:1, FEATURES : 2 * FEATURES], in_=b_out.rearrange("(o d) -> o d", o=1))
 
         tokens = support_transport.rearrange("w k t f -> w (k t) f")
         logits_sb = {}
@@ -74,22 +68,27 @@ def tile_consensustransportmemorypool_pb_t_kernel(
             nc.sync.dma_start(out=flat_sb[h][:], in_=rows.rearrange("(p j) f -> p (j f)", j=PACK))
 
         load_logits(0)
+        load_logits(1)
         wv_sb = inputs.tile([P, FEATURE_CHUNKS * FEATURES], BF16)
         nc.sync.dma_start(
             out=wv_sb[:].rearrange("p (o k) -> p o k", o=FEATURE_CHUNKS),
             in_=Wv.rearrange("(o p) k -> p o k", p=P),
         )
-        load_flat(0)
-        load_flat(1)
-        load_logits(1)
-        load_flat(2)
-        load_flat(3)
+        for h in range(2 * UNITS_PER_CLASS):
+            load_flat(h)
+        load_logits(2)
         slots_sb = inputs.tile([P, CLASSES, FEATURES], BF16)
         nc.sync.dma_start(out=slots_sb[:], in_=class_slots.rearrange("w s d -> s w d"))
+        gain = consts.tile([P, FEATURES], BF16)
+        shift = consts.tile([P, FEATURES], BF16)
         for c in range(2, CLASSES):
-            load_logits(c)
+            if c + 1 < CLASSES:
+                load_logits(c + 1)
             load_flat(UNITS_PER_CLASS * c)
             load_flat(UNITS_PER_CLASS * c + 1)
+            if c == 2:
+                nc.sync.dma_start(out=gain[:], in_=g_out.partition_broadcast(P))
+                nc.sync.dma_start(out=shift[:], in_=b_out.partition_broadcast(P))
 
         def transpose_words(rows_sb, first_block, tag):
             words = rows_sb[:].bitcast(F32)
@@ -112,12 +111,12 @@ def tile_consensustransportmemorypool_pb_t_kernel(
         def transpose_flat(h):
             flat_banks[h] = [transpose_words(flat_sb[h], first, "ft") for first in (0, 2)]
 
-        def regroup_flat(h):
-            flat_grouped[h] = work.tile([P, PACK * UNIT_TOKENS], BF16, name="flat_grouped", align_bytes=64)
-            for half, first in enumerate((0, 2)):
-                scalar_share = h >= UNITS_PER_CLASS and h % UNITS_PER_CLASS == 0 and half == 1
-                copy = nc.scalar.copy if scalar_share else nc.vector.tensor_copy
-                regroup_words(copy, flat_grouped[h], first, flat_banks[h][half])
+        def regroup_flat(h, half):
+            if half == 0:
+                flat_grouped[h] = work.tile([P, PACK * UNIT_TOKENS], BF16, name="flat_grouped", align_bytes=64)
+            scalar_share = h >= UNITS_PER_CLASS and h % UNITS_PER_CLASS == 0 and half == 1
+            copy = nc.scalar.copy if scalar_share else nc.vector.tensor_copy
+            regroup_words(copy, flat_grouped[h], 2 * half, flat_banks[h][half])
 
         def quantise_flat(h):
             flat_codes[h] = work.tile([P, UNIT_TOKENS], U32, name="flat_codes", align_bytes=64)
@@ -228,22 +227,30 @@ def tile_consensustransportmemorypool_pb_t_kernel(
                 stop=(g == UNITS_PER_CLASS - 1),
             )
 
+        inv_sum = {}
         y = {}
+        moments = {}
         mean_var = {}
         rstd = {}
         centred = {}
 
-        def norm_stats(c):
-            inv_sum = stats.tile([P, 1], F32)
-            nc.vector.reciprocal(out=inv_sum[:], in_=row_sum[c][:])
+        def inverse_sum(c):
+            inv_sum[c] = stats.tile([P, 1], F32, name="inv_sum")
+            nc.vector.reciprocal(out=inv_sum[c][:], in_=row_sum[c][:])
+
+        def norm_residual(c):
             y[c] = work.tile([P, FEATURES], F32, name="y")
             nc.vector.scalar_tensor_tensor(
-                out=y[c][:], in0=mem_bank[c][:], scalar=inv_sum[:], in1=slots_sb[:, c, :], op0=ALU.mult, op1=ALU.add
+                out=y[c][:], in0=mem_bank[c][:], scalar=inv_sum[c][:], in1=slots_sb[:, c, :], op0=ALU.mult, op1=ALU.add
             )
-            moments = stats.tile([P, 6], F32)
-            nc.vector.bn_stats(out=moments[:], in_=y[c][:])
+
+        def norm_moments(c):
+            moments[c] = stats.tile([P, 6], F32, name="moments")
+            nc.vector.bn_stats(out=moments[c][:], in_=y[c][:])
+
+        def norm_scale(c):
             mean_var[c] = stats.tile([P, 2], F32, name="mean_var")
-            nc.vector.bn_aggr(out=mean_var[c][:], in_=moments[:])
+            nc.vector.bn_aggr(out=mean_var[c][:], in_=moments[c][:])
             var_eps = stats.tile([P, 1], F32)
             nc.gpsimd.tensor_scalar(
                 out=var_eps[:], in0=mean_var[c][:, 1:2], scalar1=LN_EPS, scalar2=1.0, op0=ALU.add, op1=ALU.mult
@@ -265,58 +272,64 @@ def tile_consensustransportmemorypool_pb_t_kernel(
             nc.sync.dma_start(out=out[c, :, :], in_=result[:])
 
         row_max(0)
+        row_max(1)
         exponentials(0)
         wv_grouped = consts.tile([P, PACK * FEATURES], BF16, align_bytes=64)
         for first in (0, 2):
             regroup_words(nc.scalar.copy, wv_grouped, first, transpose_words(wv_sb, first, "v"))
         transpose_flat(0)
-        regroup_flat(0)
+        transpose_weights(0)
+        regroup_flat(0, 0)
+        regroup_flat(0, 1)
         transpose_flat(1)
+        exponentials(1)
         wv_codes = consts.tile([P, FEATURES], U32, align_bytes=64)
         wv_scales = consts.tile([P, FEATURES], U8, align_bytes=64)
         nc.vector.quantize_mx(out=wv_codes[:].bitcast(FP8X4), scales=wv_scales[:], in_=wv_grouped[:])
         quantise_flat(0)
-        gain = consts.tile([P, FEATURES], F32)
-        shift = consts.tile([P, FEATURES], F32)
-        for i, spread in enumerate((gain, shift)):
-            bank = psum.tile([P, FEATURES], F32, tag="v", bufs=PSUM_BUFS["v"])
-            nc.tensor.matmul(
-                out=bank[:], lhsT=ones[:], rhs=affine_rows[:, i * FEATURES : (i + 1) * FEATURES], start=True, stop=True
-            )
-            nc.scalar.copy(out=spread[:], in_=bank[:])
+        regroup_weights(0)
         project(0)
-        transpose_weights(0)
-        regroup_flat(1)
+        regroup_flat(1, 0)
+        regroup_flat(1, 1)
         transpose_flat(2)
+        transpose_weights(1)
+
+        def for_unit(stage, h, *more):
+            if 0 <= h < UNITS:
+                stage(h, *more)
+
+        def for_class(stage, c):
+            if 0 <= c < CLASSES:
+                stage(c)
 
         for i in range(UNITS + 3):
-            odd = i % UNITS_PER_CLASS == 1
-            if i < UNITS:
-                regroup_v(i)
-            if i + 1 < UNITS:
-                quantise_flat(i + 1)
-            if 1 <= i <= UNITS:
-                if odd:
-                    quantise_weights((i - 1) // UNITS_PER_CLASS)
-                quantise_v(i - 1)
-            if i + 1 < UNITS:
-                project(i + 1)
-            if odd and 0 <= (i - 3) // UNITS_PER_CLASS < CLASSES:
-                norm_stats((i - 3) // UNITS_PER_CLASS)
-            if not odd and 0 <= (i - 4) // UNITS_PER_CLASS < CLASSES:
-                norm_finish((i - 4) // UNITS_PER_CLASS)
-            if not odd and i // UNITS_PER_CLASS + 1 < CLASSES:
-                row_max(i // UNITS_PER_CLASS + 1)
-            if 1 <= i <= UNITS:
-                pool_unit(i - 1)
-            if i + 2 < UNITS:
-                regroup_flat(i + 2)
-            if i + 3 < UNITS:
-                transpose_flat(i + 3)
-            if odd and (i + 1) // UNITS_PER_CLASS < CLASSES:
-                exponentials((i + 1) // UNITS_PER_CLASS)
-                transpose_weights((i + 1) // UNITS_PER_CLASS)
-            if not odd and i // UNITS_PER_CLASS < CLASSES:
-                regroup_weights(i // UNITS_PER_CLASS)
-            if odd and 0 <= (i - 3) // UNITS_PER_CLASS < CLASSES:
-                norm_centre((i - 3) // UNITS_PER_CLASS)
+            k, second = divmod(i, UNITS_PER_CLASS)
+            for_unit(regroup_v, i)
+            for_unit(quantise_flat, i + 1)
+            if second:
+                for_class(quantise_weights, k)
+            else:
+                for_class(norm_centre, k - 2)
+            for_unit(quantise_v, i - 1)
+            for_unit(project, i + 1)
+            if second:
+                for_class(norm_residual, k - 1)
+            else:
+                for_class(row_max, k + 2)
+            for_unit(regroup_flat, i + 2, 0)
+            if second:
+                for_class(norm_moments, k - 1)
+            else:
+                for_class(inverse_sum, k - 1)
+            for_unit(regroup_flat, i + 2, 1)
+            if second:
+                for_class(norm_scale, k - 1)
+            else:
+                for_class(norm_finish, k - 2)
+            for_unit(pool_unit, i - 1)
+            for_unit(transpose_flat, i + 3)
+            if second:
+                for_class(exponentials, k + 2)
+                for_class(transpose_weights, k + 2)
+            else:
+                for_class(regroup_weights, k + 1)

@@ -86,7 +86,7 @@ def tile_consensustransportmemorypool_pb_t_kernel(
                 load_logits(c + 1)
             load_flat(UNITS_PER_CLASS * c)
             load_flat(UNITS_PER_CLASS * c + 1)
-            if c == 2:
+            if c == 3:
                 nc.sync.dma_start(out=gain[:], in_=g_out.partition_broadcast(P))
                 nc.sync.dma_start(out=shift[:], in_=b_out.partition_broadcast(P))
 
@@ -183,10 +183,10 @@ def tile_consensustransportmemorypool_pb_t_kernel(
 
         def exponentials(c):
             row_sum[c] = stats.tile([P, 1], F32, name="row_sum")
-            e_sb[c] = work.tile([P, UNITS_PER_CLASS, PACK, P], BF16, name="e_sb")
+            e_sb[c] = work.tile([P, TOKENS], BF16, name="e_sb")
             nc.scalar.activation(
-                out=e_sb[c][:].rearrange("s g j p -> s g p j"),
-                in_=logits_sb[c][:].rearrange("s (g p j) -> s g p j", g=UNITS_PER_CLASS, j=PACK),
+                out=e_sb[c][:],
+                in_=logits_sb[c][:],
                 func=ACT.Exp,
                 bias=neg_max[c][:],
                 scale=1.0,
@@ -195,9 +195,10 @@ def tile_consensustransportmemorypool_pb_t_kernel(
 
         def transpose_weights(c):
             e_bank[c] = psum.tile([P, UNITS_PER_CLASS, PACK, SLOTS], BF16, name="e_bank", tag="eT", bufs=PSUM_BUFS["eT"])
+            blocks = e_sb[c][:].rearrange("s (g p j) -> s g j p", g=UNITS_PER_CLASS, j=PACK)
             for g in range(UNITS_PER_CLASS):
                 for j in range(PACK):
-                    nc.tensor.transpose(e_bank[c][:, g, j, :], e_sb[c][:, g, j, :], ident_bf16[:])
+                    nc.tensor.transpose(e_bank[c][:, g, j, :], blocks[:, g, j, :], ident_bf16[:])
 
         def regroup_weights(c):
             e_grouped[c] = work.tile([P, UNITS_PER_CLASS, SLOTS, PACK], BF16, name="e_grouped", align_bytes=64)
@@ -306,11 +307,11 @@ def tile_consensustransportmemorypool_pb_t_kernel(
             k, second = divmod(i, UNITS_PER_CLASS)
             for_unit(regroup_v, i)
             for_unit(quantise_flat, i + 1)
+            for_unit(quantise_v, i - 1)
             if second:
                 for_class(quantise_weights, k)
             else:
                 for_class(norm_centre, k - 2)
-            for_unit(quantise_v, i - 1)
             for_unit(project, i + 1)
             if second:
                 for_class(norm_residual, k - 1)

@@ -48,8 +48,6 @@ def tile_consensustransportmemorypool_pb_t_kernel(
 
         ident_f32 = consts.tile([P, P], F32)
         make_identity(nc, ident_f32[:])
-        ident_bf16 = consts.tile([P, P], BF16)
-        make_identity(nc, ident_bf16[:])
         minus_half = consts.tile([P, 1], F32)
         nc.gpsimd.memset(minus_half[:], -0.5)
 
@@ -194,15 +192,16 @@ def tile_consensustransportmemorypool_pb_t_kernel(
             )
 
         def transpose_weights(c):
-            e_bank[c] = psum.tile([P, UNITS_PER_CLASS, PACK, SLOTS], BF16, name="e_bank", tag="eT", bufs=PSUM_BUFS["eT"])
-            blocks = e_sb[c][:].rearrange("s (g p j) -> s g j p", g=UNITS_PER_CLASS, j=PACK)
+            e_bank[c] = psum.tile([P, UNITS_PER_CLASS, PACK // PAIR, SLOTS], F32, name="e_bank", tag="eT", bufs=PSUM_BUFS["eT"])
+            blocks = e_sb[c][:].bitcast(F32).rearrange("s (g p u) -> s g u p", g=UNITS_PER_CLASS, u=PACK // PAIR)
             for g in range(UNITS_PER_CLASS):
-                for j in range(PACK):
-                    nc.tensor.transpose(e_bank[c][:, g, j, :], blocks[:, g, j, :], ident_bf16[:])
+                for u in range(PACK // PAIR):
+                    nc.tensor.transpose(e_bank[c][:, g, u, :], blocks[:, g, u, :], ident_f32[:])
 
         def regroup_weights(c):
-            e_grouped[c] = work.tile([P, UNITS_PER_CLASS, SLOTS, PACK], BF16, name="e_grouped", align_bytes=64)
-            nc.scalar.copy(out=e_grouped[c][:], in_=e_bank[c][:].rearrange("p g j s -> p g s j"))
+            e_grouped[c] = work.tile([P, UNITS_PER_CLASS * SLOTS * PACK], BF16, name="e_grouped", align_bytes=64)
+            words = e_grouped[c][:].bitcast(F32).rearrange("p (g s u) -> p g s u", g=UNITS_PER_CLASS, s=SLOTS)
+            nc.scalar.copy(out=words, in_=e_bank[c][:].rearrange("p g u s -> p g s u"))
 
         def quantise_weights(c):
             e_codes[c] = work.tile([P, UNITS_PER_CLASS * SLOTS], U32, name="e_codes", align_bytes=64)
@@ -210,7 +209,7 @@ def tile_consensustransportmemorypool_pb_t_kernel(
             nc.vector.quantize_mx(
                 out=e_codes[c][:].bitcast(FP8X4),
                 scales=e_scales[c][:],
-                in_=e_grouped[c][:].rearrange("p g s j -> p (g s j)"),
+                in_=e_grouped[c][:],
             )
 
         def pool_unit(h):

@@ -112,7 +112,7 @@ def tile_consensustransportmemorypool_pb_t_kernel(
         def regroup_flat(h, half):
             if half == 0:
                 flat_grouped[h] = work.tile([P, PACK * UNIT_TOKENS], BF16, name="flat_grouped", align_bytes=64)
-            scalar_share = h >= UNITS_PER_CLASS and h % UNITS_PER_CLASS == 0 and half == 1
+            scalar_share = h >= UNITS_PER_CLASS and half == 1
             copy = nc.scalar.copy if scalar_share else nc.vector.tensor_copy
             regroup_words(copy, flat_grouped[h], 2 * half, flat_banks[h][half])
 

@@ -46,10 +46,12 @@ def tile_consensustransportmemorypool_pb_t_kernel(
         results = ctx.enter_context(tc.tile_pool(name="results", bufs=CLASSES))
         psum = ctx.enter_context(tc.psum_pool(name="psum", bufs=1))
 
-        ident_f32 = consts.tile([P, P], F32)
-        make_identity(nc, ident_f32[:])
         minus_half = consts.tile([P, 1], F32)
         nc.gpsimd.memset(minus_half[:], -0.5)
+        ident_f32 = consts.tile([P, P], F32)
+        make_identity(nc, ident_f32[:])
+        first_exp = consts.tile([P, 1], F32)
+        nc.scalar.activation(out=first_exp[:], in_=minus_half[:], func=ACT.Exp)
 
         tokens = support_transport.rearrange("w k t f -> w (k t) f")
         logits_sb = {}
@@ -59,29 +61,43 @@ def tile_consensustransportmemorypool_pb_t_kernel(
             logits_sb[c] = inputs.tile([P, TOKENS], BF16, name="logits%d" % c)
             nc.sync.dma_start(out=logits_sb[c][:], in_=logits[c, :, :])
 
-        def load_flat(h):
+        def load_flat(h, pieces=1):
             c, g = divmod(h, UNITS_PER_CLASS)
             flat_sb[h] = inputs.tile([P, PACK * FEATURES], BF16, name="flat%d" % h)
             rows = tokens[c, g * UNIT_TOKENS : (g + 1) * UNIT_TOKENS, :]
-            nc.sync.dma_start(out=flat_sb[h][:], in_=rows.rearrange("(p j) f -> p (j f)", j=PACK))
+            rows = rows.rearrange("(p j) f -> p (j f)", j=PACK)
+            width = PACK * FEATURES // pieces
+            for piece in range(pieces):
+                cols = slice(piece * width, (piece + 1) * width)
+                nc.sync.dma_start(out=flat_sb[h][:, cols], in_=rows[:, cols])
+
+        wv_sb = inputs.tile([P, FEATURE_CHUNKS * FEATURES], BF16)
+
+        def load_wv(half):
+            rows = slice(half * 2 * P, (half + 1) * 2 * P)
+            cols = slice(half * 2 * FEATURES, (half + 1) * 2 * FEATURES)
+            nc.sync.dma_start(
+                out=wv_sb[:, cols].rearrange("p (o k) -> p o k", o=2),
+                in_=Wv[rows, :].rearrange("(o p) k -> p o k", p=P),
+            )
 
         load_logits(0)
+        load_wv(0)
+        load_wv(1)
+        load_flat(0, pieces=2)
+        load_flat(1)
         load_logits(1)
-        wv_sb = inputs.tile([P, FEATURE_CHUNKS * FEATURES], BF16)
-        nc.sync.dma_start(
-            out=wv_sb[:].rearrange("p (o k) -> p o k", o=FEATURE_CHUNKS),
-            in_=Wv.rearrange("(o p) k -> p o k", p=P),
-        )
-        for h in range(2 * UNITS_PER_CLASS):
-            load_flat(h)
+        load_flat(2)
+        load_flat(3)
         load_logits(2)
+        load_flat(4)
         slots_sb = inputs.tile([P, CLASSES, FEATURES], BF16)
         nc.sync.dma_start(out=slots_sb[:], in_=class_slots.rearrange("w s d -> s w d"))
         gain = consts.tile([P, FEATURES], BF16)
         shift = consts.tile([P, FEATURES], BF16)
-        for c in range(2, CLASSES):
-            if c + 1 < CLASSES:
-                load_logits(c + 1)
+        load_flat(5)
+        for c in range(3, CLASSES):
+            load_logits(c)
             load_flat(UNITS_PER_CLASS * c)
             load_flat(UNITS_PER_CLASS * c + 1)
             if c == 3:
@@ -112,8 +128,7 @@ def tile_consensustransportmemorypool_pb_t_kernel(
         def regroup_flat(h, half):
             if half == 0:
                 flat_grouped[h] = work.tile([P, PACK * UNIT_TOKENS], BF16, name="flat_grouped", align_bytes=64)
-            scalar_share = h >= UNITS_PER_CLASS and half == 1
-            copy = nc.scalar.copy if scalar_share else nc.vector.tensor_copy
+            copy = nc.scalar.copy if half == 1 and h % 4 != 3 else nc.vector.tensor_copy
             regroup_words(copy, flat_grouped[h], 2 * half, flat_banks[h][half])
 
         def quantise_flat(h):
@@ -146,10 +161,11 @@ def tile_consensustransportmemorypool_pb_t_kernel(
                     )
                 v_banks[h].append(bank)
 
-        def regroup_v(h):
-            v_grouped[h] = work.tile([P, PACK * FEATURES], BF16, name="v_grouped", bufs=3, align_bytes=64)
+        def regroup_v(h, first_chunk):
+            if first_chunk == 0:
+                v_grouped[h] = work.tile([P, PACK * FEATURES], BF16, name="v_grouped", bufs=3, align_bytes=64)
             chunks = v_grouped[h][:].rearrange("p (c d j) -> p c d j", c=FEATURE_CHUNKS, j=PACK)
-            for chunk in range(FEATURE_CHUNKS):
+            for chunk in (first_chunk, first_chunk + 1):
                 nc.scalar.copy(out=chunks[:, chunk, :, :], in_=v_banks[h][chunk][:].rearrange("p j d -> p d j"))
 
         def quantise_v(h):
@@ -215,7 +231,8 @@ def tile_consensustransportmemorypool_pb_t_kernel(
         def pool_unit(h):
             c, g = divmod(h, UNITS_PER_CLASS)
             if g == 0:
-                mem_bank[c] = psum.tile([P, FEATURES], F32, name="mem_bank", tag="mem", bufs=PSUM_BUFS["mem"])
+                tag = "mem" if c + 1 < CLASSES else "ft"
+                mem_bank[c] = psum.tile([P, FEATURES], F32, name="mem_bank", tag=tag, bufs=PSUM_BUFS[tag])
             s_cols = slice(g * SLOTS, (g + 1) * SLOTS)
             nc.tensor.matmul_mx(
                 out=mem_bank[c][:],
@@ -272,27 +289,24 @@ def tile_consensustransportmemorypool_pb_t_kernel(
             nc.sync.dma_start(out=out[c, :, :], in_=result[:])
 
         row_max(0)
-        row_max(1)
         exponentials(0)
         wv_grouped = consts.tile([P, PACK * FEATURES], BF16, align_bytes=64)
-        for first in (0, 2):
-            regroup_words(nc.scalar.copy, wv_grouped, first, transpose_words(wv_sb, first, "v"))
+        regroup_words(nc.vector.tensor_copy, wv_grouped, 0, transpose_words(wv_sb, 0, "v"))
+        regroup_words(nc.scalar.copy, wv_grouped, 2, transpose_words(wv_sb, 2, "v"))
         transpose_flat(0)
         transpose_weights(0)
         regroup_flat(0, 0)
         regroup_flat(0, 1)
         transpose_flat(1)
-        exponentials(1)
         wv_codes = consts.tile([P, FEATURES], U32, align_bytes=64)
         wv_scales = consts.tile([P, FEATURES], U8, align_bytes=64)
         nc.vector.quantize_mx(out=wv_codes[:].bitcast(FP8X4), scales=wv_scales[:], in_=wv_grouped[:])
         quantise_flat(0)
-        regroup_weights(0)
         project(0)
         regroup_flat(1, 0)
         regroup_flat(1, 1)
         transpose_flat(2)
-        transpose_weights(1)
+        quantise_flat(1)
 
         def for_unit(stage, h, *more):
             if 0 <= h < UNITS:
@@ -302,34 +316,64 @@ def tile_consensustransportmemorypool_pb_t_kernel(
             if 0 <= c < CLASSES:
                 stage(c)
 
-        for i in range(UNITS + 3):
+        last = UNITS - 1
+        for i in range(last - 1):
             k, second = divmod(i, UNITS_PER_CLASS)
-            for_unit(regroup_v, i)
-            for_unit(quantise_flat, i + 1)
+            regroup_v(i, 0)
             for_unit(quantise_v, i - 1)
             if second:
-                for_class(quantise_weights, k)
-            else:
-                for_class(norm_centre, k - 2)
-            for_unit(project, i + 1)
-            if second:
+                quantise_weights(k)
                 for_class(norm_residual, k - 1)
             else:
-                for_class(row_max, k + 2)
+                for_class(norm_scale, k - 2)
             for_unit(regroup_flat, i + 2, 0)
+            if not second:
+                row_max(k + 1)
+            for_unit(regroup_flat, i + 2, 1)
+            regroup_v(i, 2)
+            project(i + 1)
             if second:
                 for_class(norm_moments, k - 1)
             else:
+                for_class(norm_centre, k - 2)
+            for_unit(quantise_flat, i + 2)
+            if not second:
                 for_class(inverse_sum, k - 1)
-            for_unit(regroup_flat, i + 2, 1)
-            if second:
-                for_class(norm_scale, k - 1)
-            else:
                 for_class(norm_finish, k - 2)
             for_unit(pool_unit, i - 1)
             for_unit(transpose_flat, i + 3)
             if second:
-                for_class(exponentials, k + 2)
-                for_class(transpose_weights, k + 2)
+                exponentials(k + 1)
+                transpose_weights(k + 1)
             else:
-                for_class(regroup_weights, k + 1)
+                regroup_weights(k)
+
+        c = CLASSES - 1
+        regroup_v(last - 1, 0)
+        quantise_v(last - 2)
+        pool_unit(last - 2)
+        norm_scale(c - 2)
+        regroup_v(last - 1, 2)
+        project(last)
+        inverse_sum(c - 1)
+        norm_centre(c - 2)
+        regroup_weights(c)
+        norm_residual(c - 1)
+        norm_finish(c - 2)
+        regroup_v(last, 0)
+        quantise_v(last - 1)
+        quantise_weights(c)
+        pool_unit(last - 1)
+        norm_moments(c - 1)
+        regroup_v(last, 2)
+        inverse_sum(c)
+        norm_scale(c - 1)
+        norm_centre(c - 1)
+        quantise_v(last)
+        pool_unit(last)
+        norm_residual(c)
+        norm_finish(c - 1)
+        norm_moments(c)
+        norm_scale(c)
+        norm_centre(c)
+        norm_finish(c)

@@ -30,6 +30,11 @@ WORD_HALVES = FEATURES // PAIR // P
 
 PSUM_BUFS = {"ft": 2, "v": 4, "eT": 1, "mem": 1}
 
+WARM_UP_MATMULS = 5
+
+ALL = slice(0, FEATURES)
+HALVES = (slice(0, FEATURES // 2), slice(FEATURES // 2, FEATURES))
+
 FLOPS = 2 * CLASSES * TOKENS * FEATURES * FEATURES + 2 * CLASSES * SLOTS * TOKENS * FEATURES
 
 
@@ -52,6 +57,12 @@ def tile_consensustransportmemorypool_pb_t_kernel(
         make_identity(nc, ident_f32[:])
         first_exp = consts.tile([P, 1], F32)
         nc.scalar.activation(out=first_exp[:], in_=minus_half[:], func=ACT.Exp)
+
+        zeros = consts.tile([P, FEATURES], BF16)
+        nc.vector.memset(zeros[:].bitcast(U32), 0)
+        warm_up = psum.tile([P, FEATURES], F32, name="warm_up", tag="mem", bufs=PSUM_BUFS["mem"])
+        for unused in range(WARM_UP_MATMULS):
+            nc.tensor.matmul(warm_up[:], lhsT=zeros[:, 0:P], rhs=zeros[:], start=True, stop=True)
 
         tokens = support_transport.rearrange("w k t f -> w (k t) f")
         logits_sb = {}
@@ -168,10 +179,15 @@ def tile_consensustransportmemorypool_pb_t_kernel(
             for chunk in (first_chunk, first_chunk + 1):
                 nc.scalar.copy(out=chunks[:, chunk, :, :], in_=v_banks[h][chunk][:].rearrange("p j d -> p d j"))
 
-        def quantise_v(h):
-            v_codes[h] = work.tile([P, FEATURES], U32, name="v_codes", align_bytes=64)
-            v_scales[h] = work.tile([P, FEATURES], U8, name="v_scales", align_bytes=64)
-            nc.vector.quantize_mx(out=v_codes[h][:].bitcast(FP8X4), scales=v_scales[h][:], in_=v_grouped[h][:])
+        def quantise_v(h, cols=ALL):
+            if cols.start == 0:
+                v_codes[h] = work.tile([P, FEATURES], U32, name="v_codes", align_bytes=64)
+                v_scales[h] = work.tile([P, FEATURES], U8, name="v_scales", align_bytes=64)
+            nc.vector.quantize_mx(
+                out=v_codes[h][:, cols].bitcast(FP8X4),
+                scales=v_scales[h][:, cols],
+                in_=v_grouped[h][:, PACK * cols.start : PACK * cols.stop],
+            )
 
         neg_max = {}
         row_sum = {}
@@ -228,18 +244,18 @@ def tile_consensustransportmemorypool_pb_t_kernel(
                 in_=e_grouped[c][:],
             )
 
-        def pool_unit(h):
+        def pool_unit(h, cols=ALL):
             c, g = divmod(h, UNITS_PER_CLASS)
             if g == 0:
-                tag = "mem" if c + 1 < CLASSES else "ft"
-                mem_bank[c] = psum.tile([P, FEATURES], F32, name="mem_bank", tag=tag, bufs=PSUM_BUFS[tag])
+                tag = "mem" if cols is ALL else "ft"
+                mem_bank[c, cols.start] = psum.tile([P, FEATURES], F32, name="mem_bank", tag=tag, bufs=PSUM_BUFS[tag])
             s_cols = slice(g * SLOTS, (g + 1) * SLOTS)
             nc.tensor.matmul_mx(
-                out=mem_bank[c][:],
+                out=mem_bank[c, cols.start][:, 0 : cols.stop - cols.start],
                 lhsT=e_codes[c][:, s_cols].bitcast(FP8X4),
                 lhsT_scale=e_scales[c][:, s_cols],
-                rhs=v_codes[h][:].bitcast(FP8X4),
-                rhs_scale=v_scales[h][:],
+                rhs=v_codes[h][:, cols].bitcast(FP8X4),
+                rhs_scale=v_scales[h][:, cols],
                 start=(g == 0),
                 stop=(g == UNITS_PER_CLASS - 1),
             )
@@ -255,19 +271,26 @@ def tile_consensustransportmemorypool_pb_t_kernel(
             inv_sum[c] = stats.tile([P, 1], F32, name="inv_sum")
             nc.vector.reciprocal(out=inv_sum[c][:], in_=row_sum[c][:])
 
-        def norm_residual(c):
-            y[c] = work.tile([P, FEATURES], F32, name="y")
+        def norm_residual(c, cols=ALL):
+            if cols.start == 0:
+                y[c] = work.tile([P, FEATURES], F32, name="y")
             nc.vector.scalar_tensor_tensor(
-                out=y[c][:], in0=mem_bank[c][:], scalar=inv_sum[c][:], in1=slots_sb[:, c, :], op0=ALU.mult, op1=ALU.add
+                out=y[c][:, cols],
+                in0=mem_bank[c, cols.start][:, 0 : cols.stop - cols.start],
+                scalar=inv_sum[c][:],
+                in1=slots_sb[:, c, cols],
+                op0=ALU.mult,
+                op1=ALU.add,
             )
 
-        def norm_moments(c):
-            moments[c] = stats.tile([P, 6], F32, name="moments")
-            nc.vector.bn_stats(out=moments[c][:], in_=y[c][:])
+        def norm_moments(c, parts=(ALL,)):
+            moments[c] = stats.tile([P, len(parts), 6], F32, name="moments%d" % len(parts))
+            for part, cols in enumerate(parts):
+                nc.vector.bn_stats(out=moments[c][:, part, :], in_=y[c][:, cols])
 
         def norm_scale(c):
             mean_var[c] = stats.tile([P, 2], F32, name="mean_var")
-            nc.vector.bn_aggr(out=mean_var[c][:], in_=moments[c][:])
+            nc.vector.bn_aggr(out=mean_var[c][:], in_=moments[c][:].rearrange("p n s -> p (n s)"))
             var_eps = stats.tile([P, 1], F32)
             nc.gpsimd.tensor_scalar(
                 out=var_eps[:], in0=mean_var[c][:, 1:2], scalar1=LN_EPS, scalar2=1.0, op0=ALU.add, op1=ALU.mult
@@ -281,12 +304,18 @@ def tile_consensustransportmemorypool_pb_t_kernel(
                 out=centred[c][:], in0=y[c][:], scalar=mean_var[c][:, 0:1], in1=gain[:], op0=ALU.subtract, op1=ALU.mult
             )
 
-        def norm_finish(c):
+        def norm_finish(c, parts=(ALL,)):
             result = results.tile([P, FEATURES], F32)
-            nc.vector.scalar_tensor_tensor(
-                out=result[:], in0=centred[c][:], scalar=rstd[c][:], in1=shift[:], op0=ALU.mult, op1=ALU.add
-            )
-            nc.sync.dma_start(out=out[c, :, :], in_=result[:])
+            for cols in parts:
+                nc.vector.scalar_tensor_tensor(
+                    out=result[:, cols],
+                    in0=centred[c][:, cols],
+                    scalar=rstd[c][:],
+                    in1=shift[:, cols],
+                    op0=ALU.mult,
+                    op1=ALU.add,
+                )
+                nc.sync.dma_start(out=out[c, :, cols], in_=result[:, cols])
 
         row_max(0)
         exponentials(0)
@@ -294,7 +323,6 @@ def tile_consensustransportmemorypool_pb_t_kernel(
         regroup_words(nc.vector.tensor_copy, wv_grouped, 0, transpose_words(wv_sb, 0, "v"))
         regroup_words(nc.scalar.copy, wv_grouped, 2, transpose_words(wv_sb, 2, "v"))
         transpose_flat(0)
-        transpose_weights(0)
         regroup_flat(0, 0)
         regroup_flat(0, 1)
         transpose_flat(1)
@@ -306,6 +334,7 @@ def tile_consensustransportmemorypool_pb_t_kernel(
         regroup_flat(1, 0)
         regroup_flat(1, 1)
         transpose_flat(2)
+        transpose_weights(0)
         quantise_flat(1)
 
         def for_unit(stage, h, *more):
@@ -363,17 +392,21 @@ def tile_consensustransportmemorypool_pb_t_kernel(
         regroup_v(last, 0)
         quantise_v(last - 1)
         quantise_weights(c)
-        pool_unit(last - 1)
+        for cols in HALVES:
+            pool_unit(last - 1, cols)
         norm_moments(c - 1)
-        regroup_v(last, 2)
         inverse_sum(c)
+        quantise_v(last, HALVES[0])
+        pool_unit(last, HALVES[0])
         norm_scale(c - 1)
+        regroup_v(last, 2)
+        norm_residual(c, HALVES[0])
         norm_centre(c - 1)
-        quantise_v(last)
-        pool_unit(last)
-        norm_residual(c)
+        quantise_v(last, HALVES[1])
+        pool_unit(last, HALVES[1])
         norm_finish(c - 1)
-        norm_moments(c)
+        norm_residual(c, HALVES[1])
+        norm_moments(c, HALVES)
         norm_scale(c)
         norm_centre(c)
-        norm_finish(c)
+        norm_finish(c, HALVES)

@@ -28,7 +28,7 @@ UNITS = CLASSES * UNITS_PER_CLASS
 FEATURE_CHUNKS = FEATURES // P
 WORD_HALVES = FEATURES // PAIR // P
 
-PSUM_BUFS = {"ft": 2, "v": 4, "eT": 1, "mem": 1}
+PSUM_BUFS = {"ft": 2, "v": 4, "class0": 1, "class1": 1}
 
 WARM_UP_MATMULS = 5
 
@@ -36,6 +36,10 @@ ALL = slice(0, FEATURES)
 HALVES = (slice(0, FEATURES // 2), slice(FEATURES // 2, FEATURES))
 
 FLOPS = 2 * CLASSES * TOKENS * FEATURES * FEATURES + 2 * CLASSES * SLOTS * TOKENS * FEATURES
+
+
+def class_tag(c):
+    return "class%d" % (c % 2)
 
 
 def tile_consensustransportmemorypool_pb_t_kernel(
@@ -60,7 +64,7 @@ def tile_consensustransportmemorypool_pb_t_kernel(
 
         zeros = consts.tile([P, FEATURES], BF16)
         nc.vector.memset(zeros[:].bitcast(U32), 0)
-        warm_up = psum.tile([P, FEATURES], F32, name="warm_up", tag="mem", bufs=PSUM_BUFS["mem"])
+        warm_up = psum.tile([P, FEATURES], F32, name="warm_up", tag="class1", bufs=PSUM_BUFS["class1"])
         for unused in range(WARM_UP_MATMULS):
             nc.tensor.matmul(warm_up[:], lhsT=zeros[:, 0:P], rhs=zeros[:], start=True, stop=True)
 
@@ -154,9 +158,8 @@ def tile_consensustransportmemorypool_pb_t_kernel(
         v_codes = {}
         v_scales = {}
 
-        def project(h):
-            v_banks[h] = []
-            for chunk in range(FEATURE_CHUNKS):
+        def project(h, chunks=range(FEATURE_CHUNKS)):
+            for chunk in chunks:
                 d_cols = slice(chunk * P, (chunk + 1) * P)
                 bank = psum.tile([P, PACK, P], F32, tag="v", bufs=PSUM_BUFS["v"])
                 for j in range(PACK):
@@ -170,14 +173,14 @@ def tile_consensustransportmemorypool_pb_t_kernel(
                         start=True,
                         stop=True,
                     )
-                v_banks[h].append(bank)
+                v_banks[h, chunk] = bank
 
-        def regroup_v(h, first_chunk):
-            if first_chunk == 0:
+        def regroup_v(h, chunks):
+            if 0 in chunks:
                 v_grouped[h] = work.tile([P, PACK * FEATURES], BF16, name="v_grouped", bufs=3, align_bytes=64)
-            chunks = v_grouped[h][:].rearrange("p (c d j) -> p c d j", c=FEATURE_CHUNKS, j=PACK)
-            for chunk in (first_chunk, first_chunk + 1):
-                nc.scalar.copy(out=chunks[:, chunk, :, :], in_=v_banks[h][chunk][:].rearrange("p j d -> p d j"))
+            grouped = v_grouped[h][:].rearrange("p (c d j) -> p c d j", c=FEATURE_CHUNKS, j=PACK)
+            for chunk in chunks:
+                nc.scalar.copy(out=grouped[:, chunk, :, :], in_=v_banks[h, chunk][:].rearrange("p j d -> p d j"))
 
         def quantise_v(h, cols=ALL):
             if cols.start == 0:
@@ -224,7 +227,8 @@ def tile_consensustransportmemorypool_pb_t_kernel(
             )
 
         def transpose_weights(c):
-            e_bank[c] = psum.tile([P, UNITS_PER_CLASS, PACK // PAIR, SLOTS], F32, name="e_bank", tag="eT", bufs=PSUM_BUFS["eT"])
+            tag = class_tag(c)
+            e_bank[c] = psum.tile([P, UNITS_PER_CLASS, PACK // PAIR, SLOTS], F32, name="e_bank", tag=tag, bufs=PSUM_BUFS[tag])
             blocks = e_sb[c][:].bitcast(F32).rearrange("s (g p u) -> s g u p", g=UNITS_PER_CLASS, u=PACK // PAIR)
             for g in range(UNITS_PER_CLASS):
                 for u in range(PACK // PAIR):
@@ -247,7 +251,7 @@ def tile_consensustransportmemorypool_pb_t_kernel(
         def pool_unit(h, cols=ALL):
             c, g = divmod(h, UNITS_PER_CLASS)
             if g == 0:
-                tag = "mem" if cols is ALL else "ft"
+                tag = class_tag(c) if cols is ALL else "ft"
                 mem_bank[c, cols.start] = psum.tile([P, FEATURES], F32, name="mem_bank", tag=tag, bufs=PSUM_BUFS[tag])
             s_cols = slice(g * SLOTS, (g + 1) * SLOTS)
             nc.tensor.matmul_mx(
@@ -348,28 +352,28 @@ def tile_consensustransportmemorypool_pb_t_kernel(
         last = UNITS - 1
         for i in range(last - 1):
             k, second = divmod(i, UNITS_PER_CLASS)
-            regroup_v(i, 0)
+            regroup_v(i, (0, 1, 2))
             for_unit(quantise_v, i - 1)
             if second:
                 quantise_weights(k)
                 for_class(norm_residual, k - 1)
             else:
                 for_class(norm_scale, k - 2)
-            for_unit(regroup_flat, i + 2, 0)
-            if not second:
                 row_max(k + 1)
+            for_unit(regroup_flat, i + 2, 0)
             for_unit(regroup_flat, i + 2, 1)
-            regroup_v(i, 2)
-            project(i + 1)
+            project(i + 1, (0, 1, 2))
+            for_unit(pool_unit, i - 1)
+            regroup_v(i, (3,))
+            project(i + 1, (3,))
             if second:
                 for_class(norm_moments, k - 1)
             else:
                 for_class(norm_centre, k - 2)
+                for_class(inverse_sum, k - 1)
             for_unit(quantise_flat, i + 2)
             if not second:
-                for_class(inverse_sum, k - 1)
                 for_class(norm_finish, k - 2)
-            for_unit(pool_unit, i - 1)
             for_unit(transpose_flat, i + 3)
             if second:
                 exponentials(k + 1)
@@ -378,18 +382,18 @@ def tile_consensustransportmemorypool_pb_t_kernel(
                 regroup_weights(k)
 
         c = CLASSES - 1
-        regroup_v(last - 1, 0)
+        regroup_v(last - 1, (0, 1))
         quantise_v(last - 2)
         pool_unit(last - 2)
         norm_scale(c - 2)
-        regroup_v(last - 1, 2)
+        regroup_v(last - 1, (2, 3))
         project(last)
         inverse_sum(c - 1)
         norm_centre(c - 2)
         regroup_weights(c)
         norm_residual(c - 1)
         norm_finish(c - 2)
-        regroup_v(last, 0)
+        regroup_v(last, (0, 1))
         quantise_v(last - 1)
         quantise_weights(c)
         for cols in HALVES:
@@ -399,7 +403,7 @@ def tile_consensustransportmemorypool_pb_t_kernel(
         quantise_v(last, HALVES[0])
         pool_unit(last, HALVES[0])
         norm_scale(c - 1)
-        regroup_v(last, 2)
+        regroup_v(last, (2, 3))
         norm_residual(c, HALVES[0])
         norm_centre(c - 1)
         quantise_v(last, HALVES[1])

@@ -143,7 +143,8 @@ def tile_consensustransportmemorypool_pb_t_kernel(
         def regroup_flat(h, half):
             if half == 0:
                 flat_grouped[h] = work.tile([P, PACK * UNIT_TOKENS], BF16, name="flat_grouped", align_bytes=64)
-            copy = nc.scalar.copy if half == 1 and h % 4 != 3 else nc.vector.tensor_copy
+            scalar_helps = h < UNITS_PER_CLASS or h >= UNITS_PER_CLASS * 3
+            copy = nc.scalar.copy if half == 1 and scalar_helps else nc.vector.tensor_copy
             regroup_words(copy, flat_grouped[h], 2 * half, flat_banks[h][half])
 
         def quantise_flat(h):
@@ -175,12 +176,12 @@ def tile_consensustransportmemorypool_pb_t_kernel(
                     )
                 v_banks[h, chunk] = bank
 
-        def regroup_v(h, chunks):
+        def regroup_v(h, chunks, copy=nc.scalar.copy):
             if 0 in chunks:
                 v_grouped[h] = work.tile([P, PACK * FEATURES], BF16, name="v_grouped", bufs=3, align_bytes=64)
             grouped = v_grouped[h][:].rearrange("p (c d j) -> p c d j", c=FEATURE_CHUNKS, j=PACK)
             for chunk in chunks:
-                nc.scalar.copy(out=grouped[:, chunk, :, :], in_=v_banks[h, chunk][:].rearrange("p j d -> p d j"))
+                copy(out=grouped[:, chunk, :, :], in_=v_banks[h, chunk][:].rearrange("p j d -> p d j"))
 
         def quantise_v(h, cols=ALL):
             if cols.start == 0:
@@ -267,7 +268,8 @@ def tile_consensustransportmemorypool_pb_t_kernel(
         inv_sum = {}
         y = {}
         moments = {}
-        mean_var = {}
+        mean = {}
+        neg_mean = {}
         rstd = {}
         centred = {}
 
@@ -287,25 +289,66 @@ def tile_consensustransportmemorypool_pb_t_kernel(
                 op1=ALU.add,
             )
 
+        def norm_residual_and_mean(c):
+            y[c] = work.tile([P, FEATURES], F32, name="y")
+            y_sum = stats.tile([P, 1], F32)
+            nc.vector.scalar_tensor_tensor(
+                out=y[c][:],
+                in0=mem_bank[c, 0][:],
+                scalar=inv_sum[c][:],
+                in1=slots_sb[:, c, :],
+                op0=ALU.mult,
+                op1=ALU.add,
+                accum_out=y_sum[:],
+            )
+            neg_mean[c] = stats.tile([P, 1], F32, name="neg_mean")
+            nc.gpsimd.tensor_scalar(
+                out=neg_mean[c][:], in0=y_sum[:], scalar1=-1.0 / FEATURES, scalar2=0.0, op0=ALU.mult, op1=ALU.add
+            )
+
+        def norm_squares(c):
+            squares = work.tile([P, FEATURES], F32)
+            square_sum = stats.tile([P, 1], F32)
+            nc.scalar.activation(
+                out=squares[:], in_=y[c][:], func=ACT.Square, bias=neg_mean[c][:], scale=1.0, accum_out=square_sum[:]
+            )
+            norm_rstd(c, square_sum[:], 1.0 / FEATURES)
+
         def norm_moments(c, parts=(ALL,)):
             moments[c] = stats.tile([P, len(parts), 6], F32, name="moments%d" % len(parts))
             for part, cols in enumerate(parts):
                 nc.vector.bn_stats(out=moments[c][:, part, :], in_=y[c][:, cols])
 
-        def norm_scale(c):
-            mean_var[c] = stats.tile([P, 2], F32, name="mean_var")
-            nc.vector.bn_aggr(out=mean_var[c][:], in_=moments[c][:].rearrange("p n s -> p (n s)"))
+        def norm_rstd(c, variance, factor):
             var_eps = stats.tile([P, 1], F32)
             nc.gpsimd.tensor_scalar(
-                out=var_eps[:], in0=mean_var[c][:, 1:2], scalar1=LN_EPS, scalar2=1.0, op0=ALU.add, op1=ALU.mult
+                out=var_eps[:], in0=variance, scalar1=factor, scalar2=LN_EPS, op0=ALU.mult, op1=ALU.add
             )
             rstd[c] = stats.tile([P, 1], F32, name="rstd")
             nc.gpsimd.tensor_tensor(out=rstd[c][:], in0=var_eps[:], in1=minus_half[:], op=ALU.pow)
 
-        def norm_centre(c):
+        def norm_scale(c):
+            mean_var = stats.tile([P, 2], F32, name="mean_var")
+            nc.vector.bn_aggr(out=mean_var[:], in_=moments[c][:].rearrange("p n s -> p (n s)"))
+            mean[c] = mean_var[:, 0:1]
+            norm_rstd(c, mean_var[:, 1:2], 1.0)
+
+        def norm_centre(c, parts=(ALL,)):
+            centred[c] = work.tile([P, FEATURES], F32, name="centred")
+            for cols in parts:
+                nc.vector.scalar_tensor_tensor(
+                    out=centred[c][:, cols],
+                    in0=y[c][:, cols],
+                    scalar=mean[c],
+                    in1=gain[:, cols],
+                    op0=ALU.subtract,
+                    op1=ALU.mult,
+                )
+
+        def norm_centre_by_sum(c):
             centred[c] = work.tile([P, FEATURES], F32, name="centred")
             nc.vector.scalar_tensor_tensor(
-                out=centred[c][:], in0=y[c][:], scalar=mean_var[c][:, 0:1], in1=gain[:], op0=ALU.subtract, op1=ALU.mult
+                out=centred[c][:], in0=y[c][:], scalar=neg_mean[c][:], in1=gain[:], op0=ALU.add, op1=ALU.mult
             )
 
         def norm_finish(c, parts=(ALL,)):
@@ -391,26 +434,24 @@ def tile_consensustransportmemorypool_pb_t_kernel(
         inverse_sum(c - 1)
         norm_centre(c - 2)
         regroup_weights(c)
-        norm_residual(c - 1)
+        norm_residual_and_mean(c - 1)
         norm_finish(c - 2)
-        regroup_v(last, (0, 1))
+        regroup_v(last, (0, 1, 2))
         quantise_v(last - 1)
         quantise_weights(c)
         for cols in HALVES:
             pool_unit(last - 1, cols)
-        norm_moments(c - 1)
+        regroup_v(last, (3,), nc.vector.tensor_copy)
         inverse_sum(c)
-        quantise_v(last, HALVES[0])
-        pool_unit(last, HALVES[0])
-        norm_scale(c - 1)
-        regroup_v(last, (2, 3))
-        norm_residual(c, HALVES[0])
-        norm_centre(c - 1)
-        quantise_v(last, HALVES[1])
-        pool_unit(last, HALVES[1])
-        norm_finish(c - 1)
-        norm_residual(c, HALVES[1])
+        for cols in HALVES:
+            quantise_v(last, cols)
+            pool_unit(last, cols)
+        norm_squares(c - 1)
+        norm_centre_by_sum(c - 1)
+        for cols in HALVES:
+            norm_residual(c, cols)
         norm_moments(c, HALVES)
         norm_scale(c)
-        norm_centre(c)
+        norm_finish(c - 1)
+        norm_centre(c, HALVES)
         norm_finish(c, HALVES)

from contextlib import ExitStack

import concourse.mybir as mybir
from concourse.masks import make_identity

F32 = mybir.dt.float32
BF16 = mybir.dt.bfloat16
U32 = mybir.dt.uint32
U8 = mybir.dt.uint8
FP8X4 = mybir.dt.float8_e4m3fn_x4
ALU = mybir.AluOpType
ACT = mybir.ActivationFunctionType

P = 128
PACK = 4
K_PASS = P * PACK
PAIR = 2

CLASSES = 8
SLOTS = 128
TOKENS = 1024
FEATURES = 512
LN_EPS = 1e-5

UNIT_TOKENS = K_PASS
UNITS_PER_CLASS = TOKENS // UNIT_TOKENS
UNITS = CLASSES * UNITS_PER_CLASS
FEATURE_CHUNKS = FEATURES // P
WORD_HALVES = FEATURES // PAIR // P

PSUM_BUFS = {"ft": 2, "v": 4, "class0": 1, "class1": 1}

WARM_UP_MATMULS = 5

ALL = slice(0, FEATURES)
HALVES = (slice(0, FEATURES // 2), slice(FEATURES // 2, FEATURES))

FLOPS = 2 * CLASSES * TOKENS * FEATURES * FEATURES + 2 * CLASSES * SLOTS * TOKENS * FEATURES


def class_tag(c):
    return "class%d" % (c % 2)


def tile_consensustransportmemorypool_pb_t_kernel(
    tc, logits, support_transport, Wv, class_slots, g_out, b_out, out
):
    nc = tc.nc
    with ExitStack() as ctx:
        ctx.enter_context(tc.manual_schedule())
        consts = ctx.enter_context(tc.tile_pool(name="consts", bufs=1))
        inputs = ctx.enter_context(tc.tile_pool(name="inputs", bufs=1))
        work = ctx.enter_context(tc.tile_pool(name="work", bufs=2))
        stats = ctx.enter_context(tc.tile_pool(name="stats", bufs=4))
        results = ctx.enter_context(tc.tile_pool(name="results", bufs=CLASSES))
        psum = ctx.enter_context(tc.psum_pool(name="psum", bufs=1))

        minus_half = consts.tile([P, 1], F32)
        nc.gpsimd.memset(minus_half[:], -0.5)
        ident_f32 = consts.tile([P, P], F32)
        make_identity(nc, ident_f32[:])
        first_exp = consts.tile([P, 1], F32)
        nc.scalar.activation(out=first_exp[:], in_=minus_half[:], func=ACT.Exp)

        zeros = consts.tile([P, FEATURES], BF16)
        nc.vector.memset(zeros[:].bitcast(U32), 0)
        warm_up = psum.tile([P, FEATURES], F32, name="warm_up", tag="class1", bufs=PSUM_BUFS["class1"])
        for unused in range(WARM_UP_MATMULS):
            nc.tensor.matmul(warm_up[:], lhsT=zeros[:, 0:P], rhs=zeros[:], start=True, stop=True)

        tokens = support_transport.rearrange("w k t f -> w (k t) f")
        logits_sb = {}
        flat_sb = {}

        def load_logits(c):
            logits_sb[c] = inputs.tile([P, TOKENS], BF16, name="logits%d" % c)
            nc.sync.dma_start(out=logits_sb[c][:], in_=logits[c, :, :])

        def load_flat(h, pieces=1):
            c, g = divmod(h, UNITS_PER_CLASS)
            flat_sb[h] = inputs.tile([P, PACK * FEATURES], BF16, name="flat%d" % h)
            rows = tokens[c, g * UNIT_TOKENS : (g + 1) * UNIT_TOKENS, :]
            rows = rows.rearrange("(p j) f -> p (j f)", j=PACK)
            width = PACK * FEATURES // pieces
            for piece in range(pieces):
                cols = slice(piece * width, (piece + 1) * width)
                nc.sync.dma_start(out=flat_sb[h][:, cols], in_=rows[:, cols])

        wv_sb = inputs.tile([P, FEATURE_CHUNKS * FEATURES], BF16)

        def load_wv(half):
            rows = slice(half * 2 * P, (half + 1) * 2 * P)
            cols = slice(half * 2 * FEATURES, (half + 1) * 2 * FEATURES)
            nc.sync.dma_start(
                out=wv_sb[:, cols].rearrange("p (o k) -> p o k", o=2),
                in_=Wv[rows, :].rearrange("(o p) k -> p o k", p=P),
            )

        load_logits(0)
        load_wv(0)
        load_wv(1)
        load_flat(0, pieces=2)
        load_flat(1)
        load_logits(1)
        load_flat(2)
        load_flat(3)
        load_logits(2)
        load_flat(4)
        slots_sb = inputs.tile([P, CLASSES, FEATURES], BF16)
        nc.sync.dma_start(out=slots_sb[:], in_=class_slots.rearrange("w s d -> s w d"))
        gain = consts.tile([P, FEATURES], BF16)
        shift = consts.tile([P, FEATURES], BF16)
        load_flat(5)
        for c in range(3, CLASSES):
            load_logits(c)
            load_flat(UNITS_PER_CLASS * c)
            load_flat(UNITS_PER_CLASS * c + 1)
            if c == 3:
                nc.sync.dma_start(out=gain[:], in_=g_out.partition_broadcast(P))
                nc.sync.dma_start(out=shift[:], in_=b_out.partition_broadcast(P))

        def transpose_words(rows_sb, first_block, tag):
            words = rows_sb[:].bitcast(F32)
            bank = psum.tile([P, 2, WORD_HALVES, P], F32, tag=tag, bufs=PSUM_BUFS[tag])
            for b in range(2):
                for u in range(WORD_HALVES):
                    col = ((first_block + b) * WORD_HALVES + u) * P
                    nc.tensor.transpose(bank[:, b, u, :], words[:, col : col + P], ident_f32[:])
            return bank

        def regroup_words(copy, grouped, first_block, bank):
            words = grouped[:].bitcast(F32).rearrange("q (b r u) -> q b r u", r=P, u=WORD_HALVES)
            copy(out=words[:, first_block : first_block + 2, :, :], in_=bank[:].rearrange("q b u r -> q b r u"))

        flat_banks = {}
        flat_grouped = {}
        flat_codes = {}
        flat_scales = {}

        def transpose_flat(h):
            flat_banks[h] = [transpose_words(flat_sb[h], first, "ft") for first in (0, 2)]

        def regroup_flat(h, half):
            if half == 0:
                flat_grouped[h] = work.tile([P, PACK * UNIT_TOKENS], BF16, name="flat_grouped", align_bytes=64)
            scalar_helps = h < UNITS_PER_CLASS or h >= UNITS_PER_CLASS * 3
            copy = nc.scalar.copy if half == 1 and scalar_helps else nc.vector.tensor_copy
            regroup_words(copy, flat_grouped[h], 2 * half, flat_banks[h][half])

        def quantise_flat(h):
            flat_codes[h] = work.tile([P, UNIT_TOKENS], U32, name="flat_codes", align_bytes=64)
            flat_scales[h] = work.tile([P, UNIT_TOKENS], U8, name="flat_scales", align_bytes=64)
            nc.vector.quantize_mx(
                out=flat_codes[h][:].bitcast(FP8X4), scales=flat_scales[h][:], in_=flat_grouped[h][:]
            )

        v_banks = {}
        v_grouped = {}
        v_codes = {}
        v_scales = {}

        def project(h, chunks=range(FEATURE_CHUNKS)):
            for chunk in chunks:
                d_cols = slice(chunk * P, (chunk + 1) * P)
                bank = psum.tile([P, PACK, P], F32, tag="v", bufs=PSUM_BUFS["v"])
                for j in range(PACK):
                    t_cols = slice(j * P, (j + 1) * P)
                    nc.tensor.matmul_mx(
                        out=bank[:, j, :],
                        lhsT=flat_codes[h][:, t_cols].bitcast(FP8X4),
                        lhsT_scale=flat_scales[h][:, t_cols],
                        rhs=wv_codes[:, d_cols].bitcast(FP8X4),
                        rhs_scale=wv_scales[:, d_cols],
                        start=True,
                        stop=True,
                    )
                v_banks[h, chunk] = bank

        def regroup_v(h, chunks, copy=nc.scalar.copy):
            if 0 in chunks:
                v_grouped[h] = work.tile([P, PACK * FEATURES], BF16, name="v_grouped", bufs=3, align_bytes=64)
            grouped = v_grouped[h][:].rearrange("p (c d j) -> p c d j", c=FEATURE_CHUNKS, j=PACK)
            for chunk in chunks:
                copy(out=grouped[:, chunk, :, :], in_=v_banks[h, chunk][:].rearrange("p j d -> p d j"))

        def quantise_v(h, cols=ALL):
            if cols.start == 0:
                v_codes[h] = work.tile([P, FEATURES], U32, name="v_codes", align_bytes=64)
                v_scales[h] = work.tile([P, FEATURES], U8, name="v_scales", align_bytes=64)
            nc.vector.quantize_mx(
                out=v_codes[h][:, cols].bitcast(FP8X4),
                scales=v_scales[h][:, cols],
                in_=v_grouped[h][:, PACK * cols.start : PACK * cols.stop],
            )

        neg_max = {}
        row_sum = {}
        e_sb = {}
        e_bank = {}
        e_grouped = {}
        e_codes = {}
        e_scales = {}
        mem_bank = {}

        def row_max(c):
            neg_max[c] = stats.tile([P, 1], F32, name="neg_max")
            neg_logits = work.tile([P, TOKENS], BF16)
            nc.vector.tensor_scalar(
                out=neg_logits[:],
                in0=logits_sb[c][:],
                scalar1=-1.0,
                scalar2=None,
                op0=ALU.mult,
                op1=ALU.min,
                accum_out=neg_max[c][:],
            )

        def exponentials(c):
            row_sum[c] = stats.tile([P, 1], F32, name="row_sum")
            e_sb[c] = work.tile([P, TOKENS], BF16, name="e_sb")
            nc.scalar.activation(
                out=e_sb[c][:],
                in_=logits_sb[c][:],
                func=ACT.Exp,
                bias=neg_max[c][:],
                scale=1.0,
                accum_out=row_sum[c][:],
            )

        def transpose_weights(c):
            tag = class_tag(c)
            e_bank[c] = psum.tile([P, UNITS_PER_CLASS, PACK // PAIR, SLOTS], F32, name="e_bank", tag=tag, bufs=PSUM_BUFS[tag])
            blocks = e_sb[c][:].bitcast(F32).rearrange("s (g p u) -> s g u p", g=UNITS_PER_CLASS, u=PACK // PAIR)
            for g in range(UNITS_PER_CLASS):
                for u in range(PACK // PAIR):
                    nc.tensor.transpose(e_bank[c][:, g, u, :], blocks[:, g, u, :], ident_f32[:])

        def regroup_weights(c):
            e_grouped[c] = work.tile([P, UNITS_PER_CLASS * SLOTS * PACK], BF16, name="e_grouped", align_bytes=64)
            words = e_grouped[c][:].bitcast(F32).rearrange("p (g s u) -> p g s u", g=UNITS_PER_CLASS, s=SLOTS)
            nc.scalar.copy(out=words, in_=e_bank[c][:].rearrange("p g u s -> p g s u"))

        def quantise_weights(c):
            e_codes[c] = work.tile([P, UNITS_PER_CLASS * SLOTS], U32, name="e_codes", align_bytes=64)
            e_scales[c] = work.tile([P, UNITS_PER_CLASS * SLOTS], U8, name="e_scales", align_bytes=64)
            nc.vector.quantize_mx(
                out=e_codes[c][:].bitcast(FP8X4),
                scales=e_scales[c][:],
                in_=e_grouped[c][:],
            )

        def pool_unit(h, cols=ALL):
            c, g = divmod(h, UNITS_PER_CLASS)
            if g == 0:
                tag = class_tag(c) if cols is ALL else "ft"
                mem_bank[c, cols.start] = psum.tile([P, FEATURES], F32, name="mem_bank", tag=tag, bufs=PSUM_BUFS[tag])
            s_cols = slice(g * SLOTS, (g + 1) * SLOTS)
            nc.tensor.matmul_mx(
                out=mem_bank[c, cols.start][:, 0 : cols.stop - cols.start],
                lhsT=e_codes[c][:, s_cols].bitcast(FP8X4),
                lhsT_scale=e_scales[c][:, s_cols],
                rhs=v_codes[h][:, cols].bitcast(FP8X4),
                rhs_scale=v_scales[h][:, cols],
                start=(g == 0),
                stop=(g == UNITS_PER_CLASS - 1),
            )

        inv_sum = {}
        y = {}
        moments = {}
        mean = {}
        neg_mean = {}
        rstd = {}
        centred = {}

        def inverse_sum(c):
            inv_sum[c] = stats.tile([P, 1], F32, name="inv_sum")
            nc.vector.reciprocal(out=inv_sum[c][:], in_=row_sum[c][:])

        def norm_residual(c, cols=ALL):
            if cols.start == 0:
                y[c] = work.tile([P, FEATURES], F32, name="y")
            nc.vector.scalar_tensor_tensor(
                out=y[c][:, cols],
                in0=mem_bank[c, cols.start][:, 0 : cols.stop - cols.start],
                scalar=inv_sum[c][:],
                in1=slots_sb[:, c, cols],
                op0=ALU.mult,
                op1=ALU.add,
            )

        def norm_residual_and_mean(c):
            y[c] = work.tile([P, FEATURES], F32, name="y")
            y_sum = stats.tile([P, 1], F32)
            nc.vector.scalar_tensor_tensor(
                out=y[c][:],
                in0=mem_bank[c, 0][:],
                scalar=inv_sum[c][:],
                in1=slots_sb[:, c, :],
                op0=ALU.mult,
                op1=ALU.add,
                accum_out=y_sum[:],
            )
            neg_mean[c] = stats.tile([P, 1], F32, name="neg_mean")
            nc.gpsimd.tensor_scalar(
                out=neg_mean[c][:], in0=y_sum[:], scalar1=-1.0 / FEATURES, scalar2=0.0, op0=ALU.mult, op1=ALU.add
            )

        def norm_squares(c):
            squares = work.tile([P, FEATURES], F32)
            square_sum = stats.tile([P, 1], F32)
            nc.scalar.activation(
                out=squares[:], in_=y[c][:], func=ACT.Square, bias=neg_mean[c][:], scale=1.0, accum_out=square_sum[:]
            )
            norm_rstd(c, square_sum[:], 1.0 / FEATURES)

        def norm_moments(c, parts=(ALL,)):
            moments[c] = stats.tile([P, len(parts), 6], F32, name="moments%d" % len(parts))
            for part, cols in enumerate(parts):
                nc.vector.bn_stats(out=moments[c][:, part, :], in_=y[c][:, cols])

        def norm_rstd(c, variance, factor):
            var_eps = stats.tile([P, 1], F32)
            nc.gpsimd.tensor_scalar(
                out=var_eps[:], in0=variance, scalar1=factor, scalar2=LN_EPS, op0=ALU.mult, op1=ALU.add
            )
            rstd[c] = stats.tile([P, 1], F32, name="rstd")
            nc.gpsimd.tensor_tensor(out=rstd[c][:], in0=var_eps[:], in1=minus_half[:], op=ALU.pow)

        def norm_scale(c):
            mean_var = stats.tile([P, 2], F32, name="mean_var")
            nc.vector.bn_aggr(out=mean_var[:], in_=moments[c][:].rearrange("p n s -> p (n s)"))
            mean[c] = mean_var[:, 0:1]
            norm_rstd(c, mean_var[:, 1:2], 1.0)

        def norm_centre(c, parts=(ALL,)):
            centred[c] = work.tile([P, FEATURES], F32, name="centred")
            for cols in parts:
                nc.vector.scalar_tensor_tensor(
                    out=centred[c][:, cols],
                    in0=y[c][:, cols],
                    scalar=mean[c],
                    in1=gain[:, cols],
                    op0=ALU.subtract,
                    op1=ALU.mult,
                )

        def norm_centre_by_sum(c):
            centred[c] = work.tile([P, FEATURES], F32, name="centred")
            nc.vector.scalar_tensor_tensor(
                out=centred[c][:], in0=y[c][:], scalar=neg_mean[c][:], in1=gain[:], op0=ALU.add, op1=ALU.mult
            )

        def norm_finish(c, parts=(ALL,)):
            result = results.tile([P, FEATURES], F32)
            for cols in parts:
                nc.vector.scalar_tensor_tensor(
                    out=result[:, cols],
                    in0=centred[c][:, cols],
                    scalar=rstd[c][:],
                    in1=shift[:, cols],
                    op0=ALU.mult,
                    op1=ALU.add,
                )
                nc.sync.dma_start(out=out[c, :, cols], in_=result[:, cols])

        row_max(0)
        exponentials(0)
        wv_grouped = consts.tile([P, PACK * FEATURES], BF16, align_bytes=64)
        regroup_words(nc.vector.tensor_copy, wv_grouped, 0, transpose_words(wv_sb, 0, "v"))
        regroup_words(nc.scalar.copy, wv_grouped, 2, transpose_words(wv_sb, 2, "v"))
        transpose_flat(0)
        regroup_flat(0, 0)
        regroup_flat(0, 1)
        transpose_flat(1)
        wv_codes = consts.tile([P, FEATURES], U32, align_bytes=64)
        wv_scales = consts.tile([P, FEATURES], U8, align_bytes=64)
        nc.vector.quantize_mx(out=wv_codes[:].bitcast(FP8X4), scales=wv_scales[:], in_=wv_grouped[:])
        quantise_flat(0)
        project(0)
        regroup_flat(1, 0)
        regroup_flat(1, 1)
        transpose_flat(2)
        transpose_weights(0)
        quantise_flat(1)

        def for_unit(stage, h, *more):
            if 0 <= h < UNITS:
                stage(h, *more)

        def for_class(stage, c):
            if 0 <= c < CLASSES:
                stage(c)

        last = UNITS - 1
        for i in range(last - 1):
            k, second = divmod(i, UNITS_PER_CLASS)
            regroup_v(i, (0, 1, 2))
            for_unit(quantise_v, i - 1)
            if second:
                quantise_weights(k)
                for_class(norm_residual, k - 1)
            else:
                for_class(norm_scale, k - 2)
                row_max(k + 1)
            for_unit(regroup_flat, i + 2, 0)
            for_unit(regroup_flat, i + 2, 1)
            project(i + 1, (0, 1, 2))
            for_unit(pool_unit, i - 1)
            regroup_v(i, (3,))
            project(i + 1, (3,))
            if second:
                for_class(norm_moments, k - 1)
            else:
                for_class(norm_centre, k - 2)
                for_class(inverse_sum, k - 1)
            for_unit(quantise_flat, i + 2)
            if not second:
                for_class(norm_finish, k - 2)
            for_unit(transpose_flat, i + 3)
            if second:
                exponentials(k + 1)
                transpose_weights(k + 1)
            else:
                regroup_weights(k)

        c = CLASSES - 1
        regroup_v(last - 1, (0, 1))
        quantise_v(last - 2)
        pool_unit(last - 2)
        norm_scale(c - 2)
        regroup_v(last - 1, (2, 3))
        project(last)
        inverse_sum(c - 1)
        norm_centre(c - 2)
        regroup_weights(c)
        norm_residual_and_mean(c - 1)
        norm_finish(c - 2)
        regroup_v(last, (0, 1, 2))
        quantise_v(last - 1)
        quantise_weights(c)
        for cols in HALVES:
            pool_unit(last - 1, cols)
        regroup_v(last, (3,), nc.vector.tensor_copy)
        inverse_sum(c)
        for cols in HALVES:
            quantise_v(last, cols)
            pool_unit(last, cols)
        norm_squares(c - 1)
        norm_centre_by_sum(c - 1)
        for cols in HALVES:
            norm_residual(c, cols)
        norm_moments(c, HALVES)
        norm_scale(c)
        norm_finish(c - 1)
        norm_centre(c, HALVES)
        norm_finish(c, HALVES)
